import numpy as np
import ml_dtypes


def mxq(x, axis, fmt="e4m3"):
    dtype, down = {"e4m3": (ml_dtypes.float8_e4m3fn, 7), "e5m2": (ml_dtypes.float8_e5m2, 14)}[fmt]
    v = np.moveaxis(np.asarray(x, np.float32).astype(ml_dtypes.bfloat16).astype(np.float64), axis, -1)
    blocks = v.reshape(v.shape[:-1] + (-1, 32))
    amax = np.abs(blocks).max(-1, keepdims=True)
    byte = np.maximum(np.where(amax > 0, np.frexp(amax)[1] - 1 + 127, 0) - down, 1)
    scale = np.exp2(byte - 127.0)
    codes = (blocks / scale).astype(np.float32).astype(dtype).astype(np.float64)
    return np.moveaxis((codes * scale).reshape(v.shape), -1, axis)


WIDE = False


def mx_kscale(k):
    if not WIDE:
        return np.ones(k)
    levels = np.array([10, -10, 5, -5, 0])
    if k % 512:
        return np.exp2(np.random.permutation(np.resize(levels, k // 32))).repeat(32)
    a = np.empty((k // 512, 16))
    for p in range(k // 512):
        a[p, :8] = np.random.permutation(np.resize(levels, 8))
        for g in range(8):
            far = levels[np.abs(levels - a[p, g]) >= 10]
            a[p, g + 8] = far[np.random.randint(len(far))]
    return np.exp2(a.ravel()).repeat(32)


BF16 = ml_dtypes.bfloat16


def bf(x):
    return np.asarray(x, np.float32).astype(BF16)


def f64(x):
    return np.asarray(x).astype(np.float64)


B, I, H, L, P, G = 4096, 1024, 256, 4, 2, 4


def sigmoid(v):
    return 1.0 / (1.0 + np.exp(-v))


def setup_inputs():
    s = mx_kscale(I)
    return {"h_below": bf(np.random.standard_normal((B, I)) * 0.3 * s),
            "gates_rec": bf(np.random.standard_normal((B, G * H)) * 0.7),
            "c": bf(np.random.standard_normal((B, H))),
            "w_ih": bf(np.random.standard_normal((G * H, I)) * 1.5 / np.sqrt(I) / s),
            "b_ih": bf(np.random.standard_normal(G * H) * 0.3),
            "b_hh": bf(np.random.standard_normal(G * H) * 0.3)}


def reference(h_below, gates_rec, c, w_ih, b_ih, b_hh):
    gates = (mxq(f64(h_below), 1, "e4m3") @ mxq(f64(w_ih), 1, "e4m3").T) + f64(b_ih) + f64(gates_rec) + f64(b_hh)
    i, f, g, o = np.split(gates, G, axis=-1)
    c_new = sigmoid(f) * f64(c) + sigmoid(i) * np.tanh(g)
    h_new = sigmoid(o) * np.tanh(c_new)
    return h_new, c_new

@@ -1,0 +1,344 @@
+from contextlib import ExitStack
+
+import concourse.mybir as mybir
+from concourse.masks import make_identity
+
+FLOPS = 2 * 4096 * 1024 * 1024
+
+F32 = mybir.dt.float32
+BF16 = mybir.dt.bfloat16
+U32 = mybir.dt.uint32
+U8 = mybir.dt.uint8
+FP8X4 = mybir.dt.float8_e4m3fn_x4
+ACT = mybir.ActivationFunctionType
+ALU = mybir.AluOpType
+
+P = 128
+B = 4096
+K = 1024
+N = 1024
+H = 256
+NT = B // P
+GT = 4
+NG = NT // GT
+NPAIR = NT // 2
+POOL_GROUPS = 6
+
+
+def tile_yourlstm_pc_t_kernel(tc, h_below, gates_rec, c, w_ih, b_ih, b_hh, out_0, out_1):
+    nc = tc.nc
+    h_v = h_below.rearrange("(p t) k -> p (t k)", t=NT)
+    r_v = gates_rec.rearrange("(p t) n -> p (t n)", t=NT)
+    c_v = c.rearrange("(p t) n -> p (t n)", t=NT)
+    oh_v = out_0.rearrange("(p t) n -> p (t n)", t=NT)
+    oc_v = out_1.rearrange("(p t) n -> p (t n)", t=NT)
+    w_v = w_ih.rearrange("(a p) k -> p a k", p=P)
+
+    with ExitStack() as ctx:
+        ctx.enter_context(tc.manual_schedule())
+        const = ctx.enter_context(tc.tile_pool(name="const", bufs=1))
+        loads = ctx.enter_context(tc.tile_pool(name="loads", bufs=6))
+        work = ctx.enter_context(tc.tile_pool(name="work", bufs=3))
+        psum = ctx.enter_context(tc.psum_pool(name="psum", bufs=1))
+
+        h_t = {}
+        r_t = {}
+        c_t = {}
+        x_t = {}
+        cn_t = {}
+        hn_t = {}
+        tp_t = {}
+        pre_t = {}
+        gq_t = {}
+        hc_t = {}
+        hs_t = {}
+        acc_t = {}
+
+        def load_rec(j):
+            if j < NPAIR:
+                r_t[j] = loads.tile([P, 2 * N], BF16, tag="rec", name="rec_sb")
+                nc.sync.dma_start(out=r_t[j][:], in_=r_v[:, j * 2 * N:(j + 1) * 2 * N])
+
+        def load_h(j):
+            if j < NPAIR:
+                h_t[j] = loads.tile([P, 2 * K], BF16, tag="h", name="h_sb")
+                nc.sync.dma_start(out=h_t[j][:], in_=h_v[:, j * 2 * K:(j + 1) * 2 * K])
+
+        def load_c(q):
+            if q < NG:
+                c_t[q] = loads.tile([P, GT * H], BF16, tag="c", bufs=4, name="c_sb")
+                nc.sync.dma_start(out=c_t[q][:], in_=c_v[:, q * GT * H:(q + 1) * GT * H])
+
+        w_sb = const.tile([P, 8 * K], BF16, name="w_sb")
+        w_sb3 = w_sb[:].rearrange("p (a k) -> p a k", a=8)
+
+        def load_w(i):
+            nc.sync.dma_start(out=w_sb3[:, 2 * i:2 * i + 2, :], in_=w_v[:, 2 * i:2 * i + 2, :])
+
+        def x3(q):
+            if q not in x_t:
+                x_t[q] = work.tile([P, GT * N], F32, tag="x", bufs=4, name="x_sb")
+            return x_t[q][:].rearrange("p (a n) -> p a n", a=GT)
+
+        ident = const.tile([P, P], F32, name="ident")
+        make_identity(nc, ident[:])
+        identb = const.tile([P, P], BF16, name="identb")
+        make_identity(nc, identb[:])
+        ones = const.tile([P, P], BF16, name="ones")
+        nc.vector.memset(ones[:], 1.0)
+        brow = const.tile([P, N], BF16, name="brow")
+        nc.vector.memset(brow[:], 0.0)
+        nc.sync.dma_start(out=brow[0:1, :], in_=b_ih.rearrange("(o n) -> o n", o=1))
+        nc.sync.dma_start(out=brow[1:2, :], in_=b_hh.rearrange("(o n) -> o n", o=1))
+        warm = const.tile([P, 1], F32, name="warm")
+        nc.vector.memset(warm[:], 0.0)
+        nc.scalar.activation(out=warm[:], in_=warm[:], func=ACT.Sigmoid)
+
+        load_rec(0)
+        for i in range(4):
+            load_w(i)
+        load_h(0)
+        load_h(1)
+        load_rec(1)
+        load_rec(2)
+        load_h(2)
+        load_h(3)
+        load_c(0)
+        load_rec(3)
+        load_h(4)
+        load_h(5)
+        load_c(1)
+
+        bias_ps = [psum.tile([P, 512], F32, name="bias%d" % i) for i in range(2)]
+        for i in range(2):
+            nc.tensor.matmul(bias_ps[i][:], lhsT=ones[:], rhs=brow[:, 512 * i:512 * (i + 1)], start=True, stop=True)
+
+        def add_bias(j, i, a0, na):
+            r3 = r_t[j][:].rearrange("p (a n) -> p a n", a=2)
+            g0 = (j % 2) * 2 + a0
+            nc.vector.tensor_tensor(
+                out=x3(j // 2)[:, g0:g0 + na, 512 * i:512 * (i + 1)],
+                in0=bias_ps[i][:].unsqueeze(1).to_broadcast([P, na, 512]),
+                in1=r3[:, a0:a0 + na, 512 * i:512 * (i + 1)],
+                op=ALU.add,
+            )
+
+        def bias_matmul(j, a):
+            pre = psum.tile([P, 512], F32, tag="tp", bufs=2, name="pre")
+            pre_t[(j, a)] = pre
+            nc.tensor.matmul(pre[:], lhsT=identb[:], rhs=r_t[j][:, a * N + 512:(a + 1) * N], start=True, stop=False)
+            nc.tensor.matmul(pre[:], lhsT=ones[:], rhs=brow[:, 512:1024], start=False, stop=True)
+
+        def bias_copy(j, a):
+            nc.scalar.copy(out=x3(j // 2)[:, (j % 2) * 2 + a, 512:1024], in_=pre_t[(j, a)][:])
+
+        def transposes(j, a):
+            words = h_t[j][:].bitcast(F32)
+            tp = psum.tile([P, 512], F32, tag="tp", bufs=2, name="tp")
+            tp_t[(j, a)] = tp
+            for jj in range(4):
+                nc.tensor.transpose(
+                    tp[:, P * jj:P * (jj + 1)],
+                    words[:, 512 * a + 256 * (jj // 2) + jj % 2:512 * a + 256 * (jj // 2 + 1):2],
+                    ident[:],
+                )
+
+        def regroup(j, a):
+            q = j // 2
+            if q not in gq_t:
+                gq_t[q] = work.tile([P, GT * K], BF16, tag="gq", bufs=2, name="gq", align_bytes=64)
+            gq_w = gq_t[q][:].bitcast(F32).rearrange("p (t g r u) -> p t g r u", t=GT, g=2, u=2)
+            nc.scalar.copy(out=gq_w[:, (j % 2) * 2 + a], in_=tp_t[(j, a)][:].rearrange("p (g u r) -> p g r u", g=2, u=2))
+
+        def quantise(q, lo, n):
+            if q not in hc_t:
+                hc_t[q] = work.tile([P, GT * 256], U32, tag="hc", name="hc", align_bytes=64)
+                hs_t[q] = work.tile([P, GT * 256], U8, tag="hs", name="hs", align_bytes=64)
+            nc.vector.quantize_mx(
+                out=hc_t[q][:, lo * 256:(lo + n) * 256].bitcast(FP8X4),
+                scales=hs_t[q][:, lo * 256:(lo + n) * 256],
+                in_=gq_t[q][:, lo * K:(lo + n) * K],
+            )
+
+        def project(j, a, nh):
+            acc = psum.tile([P, 512], F32, tag="acc", bufs=4, name="acc")
+            acc_t[(j, a, nh)] = acc
+            q = j // 2
+            for g in range(2):
+                lo = (((j % 2) * 2 + a) * 2 + g) * P
+                wlo = g * N + nh * 512
+                nc.tensor.matmul_mx(
+                    out=acc[:],
+                    lhsT=hc_t[q][:, lo:lo + P].bitcast(FP8X4),
+                    lhsT_scale=hs_t[q][:, lo:lo + P],
+                    rhs=wc[:, wlo:wlo + 512].bitcast(FP8X4),
+                    rhs_scale=ws[:, wlo:wlo + 512],
+                    start=(g == 0),
+                    stop=(g == 1),
+                )
+
+        def add_proj(j, a, nh):
+            dst = x3(j // 2)[:, (j % 2) * 2 + a, 512 * nh:512 * (nh + 1)]
+            nc.vector.tensor_tensor(out=dst, in0=acc_t[(j, a, nh)][:], in1=dst, op=ALU.add)
+
+        def activate(t):
+            xt = x3(t // GT)[:, t % GT, :]
+            nc.scalar.activation(out=xt[:, 0:512], in_=xt[:, 0:512], func=ACT.Sigmoid)
+            nc.scalar.activation(out=xt[:, 512:768], in_=xt[:, 512:768], func=ACT.Tanh)
+            nc.scalar.activation(out=xt[:, 768:1024], in_=xt[:, 768:1024], func=ACT.Sigmoid)
+
+        def out3(tiles, q, tag):
+            if q not in tiles:
+                tiles[q] = work.tile([P, GT * H], F32, tag=tag, name=tag + "_sb")
+            return tiles[q][:].rearrange("p (a n) -> p a n", a=GT)
+
+        def cell_state(t0, nt, eng):
+            q = t0 // GT
+            s = slice(t0 % GT, t0 % GT + nt)
+            x = x3(q)
+            c3 = c_t[q][:].rearrange("p (a n) -> p a n", a=GT)
+            eng.tensor_tensor(out=x[:, s, 0:256], in0=x[:, s, 0:256], in1=x[:, s, 512:768], op=ALU.mult)
+            eng.tensor_tensor(out=x[:, s, 256:512], in0=x[:, s, 256:512], in1=c3[:, s, :], op=ALU.mult)
+            eng.tensor_tensor(out=out3(cn_t, q, "cn")[:, s, :], in0=x[:, s, 0:256], in1=x[:, s, 256:512], op=ALU.add)
+
+        def cell_tanh(t0, nt):
+            q = t0 // GT
+            s = slice(t0 % GT, t0 % GT + nt)
+            nc.scalar.activation(out=x3(q)[:, s, 512:768], in_=out3(cn_t, q, "cn")[:, s, :], func=ACT.Tanh)
+
+        def hidden(t0, nt):
+            q = t0 // GT
+            s = slice(t0 % GT, t0 % GT + nt)
+            x = x3(q)
+            nc.vector.tensor_tensor(out=out3(hn_t, q, "hn")[:, s, :], in0=x[:, s, 768:1024], in1=x[:, s, 512:768], op=ALU.mult)
+
+        def store(dram, tiles, t0, nt):
+            lo = (t0 % GT) * H
+            nc.sync.dma_start(out=dram[:, t0 * H:(t0 + nt) * H], in_=tiles[t0 // GT][:, lo:lo + nt * H])
+
+        add_bias(0, 0, 0, 2)
+        add_bias(0, 1, 0, 2)
+        w_words = w_sb[:].bitcast(F32)
+        wq = const.tile([P, 2 * N * 4], BF16, name="wq", align_bytes=64)
+        wq_w = wq[:].bitcast(F32).rearrange("p (g n u) -> p g n u", g=2, u=2)
+        wc = const.tile([P, 2 * N], U32, name="wc", align_bytes=64)
+        ws = const.tile([P, 2 * N], U8, name="ws", align_bytes=64)
+        for a in range(8):
+            wtp = psum.tile([P, 512], F32, tag="acc", bufs=4, name="wtp")
+            for jj in range(4):
+                nc.tensor.transpose(
+                    wtp[:, P * jj:P * (jj + 1)],
+                    w_words[:, 512 * a + 256 * (jj // 2) + jj % 2:512 * a + 256 * (jj // 2 + 1):2],
+                    ident[:],
+                )
+            src = wtp[:].rearrange("p (g u r) -> p g r u", g=2, u=2)
+            dst = wq_w[:, :, P * a:P * (a + 1), :]
+            if a % 2 == 1:
+                nc.vector.tensor_copy(out=dst, in_=src)
+            else:
+                nc.scalar.copy(out=dst, in_=src)
+            if a % 4 == 3:
+                for g in range(2):
+                    lo = g * N + (a // 4) * 512
+                    nc.vector.quantize_mx(
+                        out=wc[:, lo:lo + 512].bitcast(FP8X4),
+                        scales=ws[:, lo:lo + 512],
+                        in_=wq[:, lo * 4:(lo + 512) * 4],
+                    )
+        for a in range(2):
+            transposes(0, a)
+            regroup(0, a)
+        quantise(0, 0, 2)
+        for a in range(2):
+            transposes(1, a)
+            regroup(1, a)
+        for a in range(2):
+            for nh in range(2):
+                project(0, a, nh)
+        add_bias(1, 0, 0, 2)
+        add_bias(1, 1, 0, 2)
+        quantise(0, 2, 2)
+
+        for j in range(NPAIR):
+            q = j // 2
+            odd = j % 2 == 1
+            load_rec(j + 4)
+            if not odd:
+                load_c(q + 2)
+            load_h(j + 6)
+            jb = j + 2
+            has = jb < NPAIR
+            more = j + 1 < NPAIR
+            by_pe = []
+            if has:
+                by_pe = [1] if jb % 2 == 0 else [0, 1]
+            if j == 0:
+                prep = [2, 3]
+            elif j == 1:
+                prep = [4, 5]
+            else:
+                prep = [j + 4] if j + 4 < NPAIR else []
+            for p in prep:
+                transposes(p, 0)
+                transposes(p, 1)
+                regroup(p, 0)
+                regroup(p, 1)
+            add_proj(j, 0, 0)
+            if more:
+                project(j + 1, 0, 0)
+            if has:
+                bias_matmul(jb, by_pe[0])
+            if j > 0:
+                activate(2 * j - 1)
+            if not odd and 1 <= q <= POOL_GROUPS:
+                cell_state(GT * (q - 1), GT, nc.gpsimd)
+            if has:
+                bias_copy(jb, by_pe[0])
+                add_bias(jb, 0, 0, 2)
+            add_proj(j, 0, 1)
+            if more:
+                project(j + 1, 0, 1)
+            if len(by_pe) == 2:
+                bias_matmul(jb, by_pe[1])
+                bias_copy(jb, by_pe[1])
+            activate(2 * j)
+            if not odd and q >= 2:
+                cell_tanh(GT * (q - 2), GT)
+                store(oc_v, cn_t, GT * (q - 2), GT)
+            add_proj(j, 1, 0)
+            if more:
+                project(j + 1, 1, 0)
+            if len(by_pe) == 1:
+                add_bias(jb, 1, 0, 1)
+            add_proj(j, 1, 1)
+            if more:
+                project(j + 1, 1, 1)
+            if j == 0:
+                quantise(1, 0, GT)
+            if odd and 2 <= q <= 5:
+                hidden(GT * (q - 2), GT)
+                store(oh_v, hn_t, GT * (q - 2), GT)
+            if j == NPAIR - 2:
+                hidden(GT * 4, GT)
+                store(oh_v, hn_t, GT * 4, GT)
+            if odd and q + 2 < NG:
+                quantise(q + 2, 0, GT)
+
+        cell_state(GT * 6, GT, nc.vector)
+        activate(NT - 1)
+        cell_tanh(GT * 6, GT)
+        store(oc_v, cn_t, GT * 6, GT)
+        hidden(GT * 5, GT)
+        store(oh_v, hn_t, GT * 5, GT)
+        cell_state(NT - 4, 2, nc.vector)
+        cell_tanh(NT - 4, 2)
+        store(oc_v, cn_t, NT - 4, 2)
+        hidden(GT * 6, GT)
+        store(oh_v, hn_t, GT * 6, GT)
+        cell_state(NT - 2, 2, nc.vector)
+        cell_tanh(NT - 2, 2)
+        store(oc_v, cn_t, NT - 2, 2)
+        hidden(NT - 4, 2)
+        store(oh_v, hn_t, NT - 4, 2)
+        hidden(NT - 2, 2)
+        store(oh_v, hn_t, NT - 2, 2)

@@ -19,10 +19,29 @@ K = 1024
 N = 1024
 H = 256
 NT = B // P
-GT = 4
-NG = NT // GT
 NPAIR = NT // 2
-POOL_GROUPS = 6
+HALF = 512
+
+GP = (1, 2)
+PE0 = (5, 7, 9, 11, 13)
+UNITS = (4, 4, 4, 4, 4, 4, 4, 2, 1, 1)
+ENG = "GGGGGGGVVV"
+ORDER = "r0 h0 w0 w1 w2 w3 r1 h1 r2 h2 r3 h3 c0 c1"
+WV = (7,)
+PB = (14, 15)
+PRR = 4.9
+PRH = 5.8
+HT = 0.9
+TD = {-3: 1.0, -2: 0.5}
+LC = 0.4
+LT = 3.2
+LH = 4.27
+TLC = 0.5
+TLT = 1.2
+TLH = 1.7
+LQ = 1.72
+LTR = 3.9
+LB = 2.0
 
 
 def tile_yourlstm_pc_t_kernel(tc, h_below, gates_rec, c, w_ih, b_ih, b_hh, out_0, out_1):
@@ -37,48 +56,37 @@ def tile_yourlstm_pc_t_kernel(tc, h_below, gates_rec, c, w_ih, b_ih, b_hh, out_0
     with ExitStack() as ctx:
         ctx.enter_context(tc.manual_schedule())
         const = ctx.enter_context(tc.tile_pool(name="const", bufs=1))
-        loads = ctx.enter_context(tc.tile_pool(name="loads", bufs=6))
+        loads = ctx.enter_context(tc.tile_pool(name="loads", bufs=5))
         work = ctx.enter_context(tc.tile_pool(name="work", bufs=3))
         psum = ctx.enter_context(tc.psum_pool(name="psum", bufs=1))
 
-        h_t = {}
-        r_t = {}
-        c_t = {}
-        x_t = {}
-        cn_t = {}
-        hn_t = {}
-        tp_t = {}
-        pre_t = {}
-        gq_t = {}
-        hc_t = {}
-        hs_t = {}
-        acc_t = {}
+        h_t, r_t, c_t, x_t, cn_t, hn_t, tp_t, pre_t, gq_t, hc_t, hs_t, acc_t = [{} for i in range(12)]
 
         def load_rec(j):
-            if j < NPAIR:
-                r_t[j] = loads.tile([P, 2 * N], BF16, tag="rec", name="rec_sb")
-                nc.sync.dma_start(out=r_t[j][:], in_=r_v[:, j * 2 * N:(j + 1) * 2 * N])
+            r_t[j] = loads.tile([P, 2 * N], BF16, tag="rec", name="rec_sb")
+            nc.sync.dma_start(out=r_t[j][:], in_=r_v[:, j * 2 * N:(j + 1) * 2 * N])
 
         def load_h(j):
-            if j < NPAIR:
-                h_t[j] = loads.tile([P, 2 * K], BF16, tag="h", name="h_sb")
-                nc.sync.dma_start(out=h_t[j][:], in_=h_v[:, j * 2 * K:(j + 1) * 2 * K])
+            h_t[j] = loads.tile([P, 2 * K], BF16, tag="h", name="h_sb")
+            nc.sync.dma_start(out=h_t[j][:], in_=h_v[:, j * 2 * K:(j + 1) * 2 * K])
 
         def load_c(q):
-            if q < NG:
-                c_t[q] = loads.tile([P, GT * H], BF16, tag="c", bufs=4, name="c_sb")
-                nc.sync.dma_start(out=c_t[q][:], in_=c_v[:, q * GT * H:(q + 1) * GT * H])
+            c_t[q] = loads.tile([P, 4 * H], BF16, tag="c", bufs=3, name="c_sb")
+            nc.sync.dma_start(out=c_t[q][:], in_=c_v[:, q * 4 * H:(q + 1) * 4 * H])
 
-        w_sb = const.tile([P, 8 * K], BF16, name="w_sb")
-        w_sb3 = w_sb[:].rearrange("p (a k) -> p a k", a=8)
+        w_t, wq_t = {}, {}
 
         def load_w(i):
-            nc.sync.dma_start(out=w_sb3[:, 2 * i:2 * i + 2, :], in_=w_v[:, 2 * i:2 * i + 2, :])
+            if 0 not in w_t:
+                w_t[0] = work.tile([P, 8 * K], BF16, tag="x", bufs=5, name="w_sb", align_bytes=64)
+            dst = w_t[0][:].rearrange("p (a k) -> p a k", a=8)
+            nc.sync.dma_start(out=dst[:, 2 * i:2 * i + 2, :], in_=w_v[:, 2 * i:2 * i + 2, :])
 
-        def x3(q):
+        def x3(t):
+            q = t // 4
             if q not in x_t:
-                x_t[q] = work.tile([P, GT * N], F32, tag="x", bufs=4, name="x_sb")
-            return x_t[q][:].rearrange("p (a n) -> p a n", a=GT)
+                x_t[q] = work.tile([P, 4 * N], F32, tag="x", bufs=5, name="x_sb", align_bytes=64)
+            return x_t[q][:].rearrange("p (a n) -> p a n", a=4)
 
         ident = const.tile([P, P], F32, name="ident")
         make_identity(nc, ident[:])
@@ -93,252 +101,240 @@ def tile_yourlstm_pc_t_kernel(tc, h_below, gates_rec, c, w_ih, b_ih, b_hh, out_0
         warm = const.tile([P, 1], F32, name="warm")
         nc.vector.memset(warm[:], 0.0)
         nc.scalar.activation(out=warm[:], in_=warm[:], func=ACT.Sigmoid)
+        wc = const.tile([P, 2 * N], U32, name="wc", align_bytes=64)
+        ws = const.tile([P, 2 * N], U8, name="ws", align_bytes=64)
+        bias_sb = const.tile([P, N], F32, name="bias_sb")
+        bias_ps = [psum.tile([P, HALF], F32, name="bias%d" % i) for i in range(2)]
 
-        load_rec(0)
-        for i in range(4):
-            load_w(i)
-        load_h(0)
-        load_h(1)
-        load_rec(1)
-        load_rec(2)
-        load_h(2)
-        load_h(3)
-        load_c(0)
-        load_rec(3)
-        load_h(4)
-        load_h(5)
-        load_c(1)
+        def bias_rows(i):
+            nc.tensor.matmul(bias_ps[i][:], lhsT=ones[:], rhs=brow[:, HALF * i:HALF * (i + 1)], start=True, stop=True)
 
-        bias_ps = [psum.tile([P, 512], F32, name="bias%d" % i) for i in range(2)]
-        for i in range(2):
-            nc.tensor.matmul(bias_ps[i][:], lhsT=ones[:], rhs=brow[:, 512 * i:512 * (i + 1)], start=True, stop=True)
+        def bias_out(i):
+            nc.scalar.copy(out=bias_sb[:, HALF * i:HALF * (i + 1)], in_=bias_ps[i][:])
 
-        def add_bias(j, i, a0, na):
+        def add_bias(eng, j, i, a0, na, pool=False):
             r3 = r_t[j][:].rearrange("p (a n) -> p a n", a=2)
-            g0 = (j % 2) * 2 + a0
-            nc.vector.tensor_tensor(
-                out=x3(j // 2)[:, g0:g0 + na, 512 * i:512 * (i + 1)],
-                in0=bias_ps[i][:].unsqueeze(1).to_broadcast([P, na, 512]),
-                in1=r3[:, a0:a0 + na, 512 * i:512 * (i + 1)],
+            s = slice(HALF * i, HALF * (i + 1))
+            row = (bias_sb[:, s] if pool else bias_ps[i][:]).unsqueeze(1).to_broadcast([P, na, HALF])
+            rec = r3[:, a0:a0 + na, s]
+            eng.tensor_tensor(
+                out=x3(2 * j)[:, (2 * j) % 4 + a0:(2 * j) % 4 + a0 + na, s],
+                in0=rec if pool else row,
+                in1=row if pool else rec,
                 op=ALU.add,
             )
 
-        def bias_matmul(j, a):
-            pre = psum.tile([P, 512], F32, tag="tp", bufs=2, name="pre")
-            pre_t[(j, a)] = pre
-            nc.tensor.matmul(pre[:], lhsT=identb[:], rhs=r_t[j][:, a * N + 512:(a + 1) * N], start=True, stop=False)
-            nc.tensor.matmul(pre[:], lhsT=ones[:], rhs=brow[:, 512:1024], start=False, stop=True)
+        def bias_matmul(j, a, i=1):
+            s = slice(HALF * i, HALF * (i + 1))
+            pre = psum.tile([P, HALF], F32, tag="tp", bufs=2, name="pre")
+            pre_t[(j, a, i)] = pre
+            nc.tensor.matmul(pre[:], lhsT=identb[:], rhs=r_t[j][:, a * N + HALF * i:a * N + HALF * (i + 1)], start=True, stop=False)
+            nc.tensor.matmul(pre[:], lhsT=ones[:], rhs=brow[:, s], start=False, stop=True)
 
-        def bias_copy(j, a):
-            nc.scalar.copy(out=x3(j // 2)[:, (j % 2) * 2 + a, 512:1024], in_=pre_t[(j, a)][:])
+        def bias_copy(j, a, i=1):
+            nc.scalar.copy(out=x3(2 * j)[:, (2 * j) % 4 + a, HALF * i:HALF * (i + 1)], in_=pre_t[(j, a, i)][:])
+
+        def four_transposes(out, words):
+            for jj in range(4):
+                lo = 256 * (jj // 2) + jj % 2
+                nc.tensor.transpose(out[:, P * jj:P * (jj + 1)], words[:, lo:256 * (jj // 2 + 1):2], ident[:])
 
         def transposes(j, a):
-            words = h_t[j][:].bitcast(F32)
-            tp = psum.tile([P, 512], F32, tag="tp", bufs=2, name="tp")
-            tp_t[(j, a)] = tp
-            for jj in range(4):
-                nc.tensor.transpose(
-                    tp[:, P * jj:P * (jj + 1)],
-                    words[:, 512 * a + 256 * (jj // 2) + jj % 2:512 * a + 256 * (jj // 2 + 1):2],
-                    ident[:],
-                )
+            tp_t[(j, a)] = psum.tile([P, HALF], F32, tag="tp", bufs=2, name="tp")
+            four_transposes(tp_t[(j, a)], h_t[j][:].bitcast(F32)[:, 512 * a:512 * (a + 1)])
 
         def regroup(j, a):
             q = j // 2
             if q not in gq_t:
-                gq_t[q] = work.tile([P, GT * K], BF16, tag="gq", bufs=2, name="gq", align_bytes=64)
-            gq_w = gq_t[q][:].bitcast(F32).rearrange("p (t g r u) -> p t g r u", t=GT, g=2, u=2)
-            nc.scalar.copy(out=gq_w[:, (j % 2) * 2 + a], in_=tp_t[(j, a)][:].rearrange("p (g u r) -> p g r u", g=2, u=2))
+                gq_t[q] = work.tile([P, 4 * K], BF16, tag="gq", bufs=3, name="gq", align_bytes=64)
+            gq_w = gq_t[q][:].bitcast(F32).rearrange("p (t g r u) -> p t g r u", t=4, g=2, u=2)
+            nc.scalar.copy(out=gq_w[:, (2 * j) % 4 + a], in_=tp_t[(j, a)][:].rearrange("p (g u r) -> p g r u", g=2, u=2))
 
-        def quantise(q, lo, n):
+        def quantise(t0, nt):
+            q = t0 // 4
             if q not in hc_t:
-                hc_t[q] = work.tile([P, GT * 256], U32, tag="hc", name="hc", align_bytes=64)
-                hs_t[q] = work.tile([P, GT * 256], U8, tag="hs", name="hs", align_bytes=64)
-            nc.vector.quantize_mx(
-                out=hc_t[q][:, lo * 256:(lo + n) * 256].bitcast(FP8X4),
-                scales=hs_t[q][:, lo * 256:(lo + n) * 256],
-                in_=gq_t[q][:, lo * K:(lo + n) * K],
-            )
+                hc_t[q] = work.tile([P, 1024], U32, tag="hc", name="hc", align_bytes=64)
+                hs_t[q] = work.tile([P, 1024], U8, tag="hs", name="hs", align_bytes=64)
+            s = slice(t0 % 4 * 256, (t0 % 4 + nt) * 256)
+            nc.vector.quantize_mx(out=hc_t[q][:, s].bitcast(FP8X4), scales=hs_t[q][:, s], in_=gq_t[q][:, t0 % 4 * K:(t0 % 4 + nt) * K])
+
+        wtp_t = {}
+
+        def w_transposes(a):
+            wtp_t[a] = psum.tile([P, HALF], F32, tag="acc", bufs=4, name="wtp")
+            four_transposes(wtp_t[a], w_t[0][:].bitcast(F32)[:, 512 * a:512 * (a + 1)])
+
+        def w_regroup(a, eng):
+            half = a // 4
+            if 0 not in wq_t:
+                wq_t[0] = work.tile([P, 8 * K], BF16, tag="x", bufs=5, name="wq", align_bytes=64)
+            dst = wq_t[0][:, half * 4 * K:(half + 1) * 4 * K].bitcast(F32).rearrange("p (g n u) -> p g n u", g=2, u=2)[:, :, P * (a % 4):P * (a % 4 + 1), :]
+            src = wtp_t[a][:].rearrange("p (g u r) -> p g r u", g=2, u=2)
+            if eng == "V":
+                nc.vector.tensor_copy(out=dst, in_=src)
+            else:
+                nc.scalar.copy(out=dst, in_=src)
+
+        def w_quantise(half):
+            s = slice(half * N, (half + 1) * N)
+            nc.vector.quantize_mx(out=wc[:, s].bitcast(FP8X4), scales=ws[:, s], in_=wq_t[0][:, half * 4 * K:(half + 1) * 4 * K])
 
         def project(j, a, nh):
-            acc = psum.tile([P, 512], F32, tag="acc", bufs=4, name="acc")
+            acc = psum.tile([P, HALF], F32, tag="acc", bufs=4, name="acc")
             acc_t[(j, a, nh)] = acc
-            q = j // 2
             for g in range(2):
-                lo = (((j % 2) * 2 + a) * 2 + g) * P
-                wlo = g * N + nh * 512
+                lo = (((2 * j) % 4 + a) * 2 + g) * P
+                wlo = nh * N + g * HALF
                 nc.tensor.matmul_mx(
                     out=acc[:],
-                    lhsT=hc_t[q][:, lo:lo + P].bitcast(FP8X4),
-                    lhsT_scale=hs_t[q][:, lo:lo + P],
-                    rhs=wc[:, wlo:wlo + 512].bitcast(FP8X4),
-                    rhs_scale=ws[:, wlo:wlo + 512],
+                    lhsT=hc_t[j // 2][:, lo:lo + P].bitcast(FP8X4),
+                    lhsT_scale=hs_t[j // 2][:, lo:lo + P],
+                    rhs=wc[:, wlo:wlo + HALF].bitcast(FP8X4),
+                    rhs_scale=ws[:, wlo:wlo + HALF],
                     start=(g == 0),
                     stop=(g == 1),
                 )
 
         def add_proj(j, a, nh):
-            dst = x3(j // 2)[:, (j % 2) * 2 + a, 512 * nh:512 * (nh + 1)]
+            dst = x3(2 * j)[:, (2 * j) % 4 + a, HALF * nh:HALF * (nh + 1)]
             nc.vector.tensor_tensor(out=dst, in0=acc_t[(j, a, nh)][:], in1=dst, op=ALU.add)
 
-        def activate(t):
-            xt = x3(t // GT)[:, t % GT, :]
-            nc.scalar.activation(out=xt[:, 0:512], in_=xt[:, 0:512], func=ACT.Sigmoid)
-            nc.scalar.activation(out=xt[:, 512:768], in_=xt[:, 512:768], func=ACT.Tanh)
-            nc.scalar.activation(out=xt[:, 768:1024], in_=xt[:, 768:1024], func=ACT.Sigmoid)
+        def sl(t0, nt):
+            return slice(t0 % 4, t0 % 4 + nt)
 
-        def out3(tiles, q, tag):
+        def act(t0, nt, lo, hi, func):
+            x = x3(t0)[:, sl(t0, nt), lo:hi]
+            nc.scalar.activation(out=x, in_=x, func=func)
+
+        def out3(tiles, t0, tag):
+            q = t0 // 4
             if q not in tiles:
-                tiles[q] = work.tile([P, GT * H], F32, tag=tag, name=tag + "_sb")
-            return tiles[q][:].rearrange("p (a n) -> p a n", a=GT)
+                tiles[q] = work.tile([P, 4 * H], F32, tag=tag, bufs=3, name=tag + "_sb")
+            return tiles[q][:].rearrange("p (a n) -> p a n", a=4)
 
-        def cell_state(t0, nt, eng):
-            q = t0 // GT
-            s = slice(t0 % GT, t0 % GT + nt)
-            x = x3(q)
-            c3 = c_t[q][:].rearrange("p (a n) -> p a n", a=GT)
-            eng.tensor_tensor(out=x[:, s, 0:256], in0=x[:, s, 0:256], in1=x[:, s, 512:768], op=ALU.mult)
-            eng.tensor_tensor(out=x[:, s, 256:512], in0=x[:, s, 256:512], in1=c3[:, s, :], op=ALU.mult)
-            eng.tensor_tensor(out=out3(cn_t, q, "cn")[:, s, :], in0=x[:, s, 0:256], in1=x[:, s, 256:512], op=ALU.add)
+        def cell_f(eng, t0, nt):
+            x = x3(t0)[:, sl(t0, nt), 256:512]
+            c3 = c_t[t0 // 4][:].rearrange("p (a n) -> p a n", a=4)
+            eng.tensor_tensor(out=x, in0=x, in1=c3[:, sl(t0, nt), :], op=ALU.mult)
+
+        def cell_i(eng, t0, nt):
+            x = x3(t0)[:, sl(t0, nt), :]
+            eng.tensor_tensor(out=x[:, :, 0:256], in0=x[:, :, 0:256], in1=x[:, :, 512:768], op=ALU.mult)
+
+        def cell_add(eng, t0, nt):
+            x = x3(t0)[:, sl(t0, nt), :]
+            eng.tensor_tensor(out=out3(cn_t, t0, "cn")[:, sl(t0, nt), :], in0=x[:, :, 0:256], in1=x[:, :, 256:512], op=ALU.add)
 
         def cell_tanh(t0, nt):
-            q = t0 // GT
-            s = slice(t0 % GT, t0 % GT + nt)
-            nc.scalar.activation(out=x3(q)[:, s, 512:768], in_=out3(cn_t, q, "cn")[:, s, :], func=ACT.Tanh)
+            x = x3(t0)[:, sl(t0, nt), 512:768]
+            nc.scalar.activation(out=x, in_=out3(cn_t, t0, "cn")[:, sl(t0, nt), :], func=ACT.Tanh)
 
-        def hidden(t0, nt):
-            q = t0 // GT
-            s = slice(t0 % GT, t0 % GT + nt)
-            x = x3(q)
-            nc.vector.tensor_tensor(out=out3(hn_t, q, "hn")[:, s, :], in0=x[:, s, 768:1024], in1=x[:, s, 512:768], op=ALU.mult)
+        def hidden(eng, t0, nt):
+            x = x3(t0)[:, sl(t0, nt), :]
+            eng.tensor_tensor(out=out3(hn_t, t0, "hn")[:, sl(t0, nt), :], in0=x[:, :, 768:1024], in1=x[:, :, 512:768], op=ALU.mult)
 
         def store(dram, tiles, t0, nt):
-            lo = (t0 % GT) * H
-            nc.sync.dma_start(out=dram[:, t0 * H:(t0 + nt) * H], in_=tiles[t0 // GT][:, lo:lo + nt * H])
+            lo = (t0 % 4) * H
+            nc.sync.dma_start(out=dram[:, t0 * H:(t0 + nt) * H], in_=tiles[t0 // 4][:, lo:lo + nt * H])
 
-        add_bias(0, 0, 0, 2)
-        add_bias(0, 1, 0, 2)
-        w_words = w_sb[:].bitcast(F32)
-        wq = const.tile([P, 2 * N * 4], BF16, name="wq", align_bytes=64)
-        wq_w = wq[:].bitcast(F32).rearrange("p (g n u) -> p g n u", g=2, u=2)
-        wc = const.tile([P, 2 * N], U32, name="wc", align_bytes=64)
-        ws = const.tile([P, 2 * N], U8, name="ws", align_bytes=64)
+        plan = []
+
+        def at(when, fn, *args):
+            plan.append((when, len(plan), fn, args))
+
+
+        for k, e in enumerate(ORDER.split()):
+            at(-9 + 0.01 * k, {"h": load_h, "r": load_rec, "w": load_w, "c": load_c}[e[0]], int(e[1:]))
+        for j in range(4, NPAIR):
+            at(j - PRR, load_rec, j)
+            at(j - PRH, load_h, j)
+            if j % 2 == 0:
+                at(j - 4.7, load_c, j // 2)
+
+        V, G = nc.vector, nc.gpsimd
+        for i in range(2):
+            at(-8, bias_rows, i)
+            at(-8, bias_out, i)
+        for a in range(2):
+            at(-7.9, transposes, 0, a)
+            at(-7.9, regroup, 0, a)
+        for i in range(2):
+            at(-7.8, add_bias, V, 0, i, 0, 2)
+        at(-7.7, quantise, 0, 2)
         for a in range(8):
-            wtp = psum.tile([P, 512], F32, tag="acc", bufs=4, name="wtp")
-            for jj in range(4):
-                nc.tensor.transpose(
-                    wtp[:, P * jj:P * (jj + 1)],
-                    w_words[:, 512 * a + 256 * (jj // 2) + jj % 2:512 * a + 256 * (jj // 2 + 1):2],
-                    ident[:],
-                )
-            src = wtp[:].rearrange("p (g u r) -> p g r u", g=2, u=2)
-            dst = wq_w[:, :, P * a:P * (a + 1), :]
-            if a % 2 == 1:
-                nc.vector.tensor_copy(out=dst, in_=src)
-            else:
-                nc.scalar.copy(out=dst, in_=src)
-            if a % 4 == 3:
-                for g in range(2):
-                    lo = g * N + (a // 4) * 512
-                    nc.vector.quantize_mx(
-                        out=wc[:, lo:lo + 512].bitcast(FP8X4),
-                        scales=ws[:, lo:lo + 512],
-                        in_=wq[:, lo * 4:(lo + 512) * 4],
-                    )
+            at(-7 + 0.25 * a, w_transposes, a)
+            at(-6.9 + 0.25 * a, w_regroup, a, "V" if a in WV else "S")
+        at(-6.1, w_quantise, 0)
         for a in range(2):
-            transposes(0, a)
-            regroup(0, a)
-        quantise(0, 0, 2)
+            at(-4.35, project, 0, a, 0)
+            at(-3.7, add_proj, 0, a, 0)
+        at(-5, w_quantise, 1)
         for a in range(2):
-            transposes(1, a)
-            regroup(1, a)
-        for a in range(2):
-            for nh in range(2):
-                project(0, a, nh)
-        add_bias(1, 0, 0, 2)
-        add_bias(1, 1, 0, 2)
-        quantise(0, 2, 2)
+            at(-2.7, project, 0, a, 1)
+            at(0.5 * a, add_proj, 0, a, 1)
+        for p in (1, 2, 3):
+            for a in range(2):
+                at(-3.0 + HT * (p - 1), transposes, p, a)
+                at(-2.9 + HT * (p - 1), regroup, p, a)
+        at(-2.8, quantise, 2, 2)
+        at(0.1, quantise, 4, 4)
+        for j in GP:
+            for i in range(2):
+                for a in range(2):
+                    at(-7 + 0.1 * j, add_bias, G, j, i, a, 1, True)
 
-        for j in range(NPAIR):
-            q = j // 2
-            odd = j % 2 == 1
-            load_rec(j + 4)
-            if not odd:
-                load_c(q + 2)
-            load_h(j + 6)
-            jb = j + 2
-            has = jb < NPAIR
-            more = j + 1 < NPAIR
-            by_pe = []
-            if has:
-                by_pe = [1] if jb % 2 == 0 else [0, 1]
-            if j == 0:
-                prep = [2, 3]
-            elif j == 1:
-                prep = [4, 5]
-            else:
-                prep = [j + 4] if j + 4 < NPAIR else []
-            for p in prep:
-                transposes(p, 0)
-                transposes(p, 1)
-                regroup(p, 0)
-                regroup(p, 1)
-            add_proj(j, 0, 0)
-            if more:
-                project(j + 1, 0, 0)
-            if has:
-                bias_matmul(jb, by_pe[0])
-            if j > 0:
-                activate(2 * j - 1)
-            if not odd and 1 <= q <= POOL_GROUPS:
-                cell_state(GT * (q - 1), GT, nc.gpsimd)
-            if has:
-                bias_copy(jb, by_pe[0])
-                add_bias(jb, 0, 0, 2)
-            add_proj(j, 0, 1)
-            if more:
-                project(j + 1, 0, 1)
-            if len(by_pe) == 2:
-                bias_matmul(jb, by_pe[1])
-                bias_copy(jb, by_pe[1])
-            activate(2 * j)
-            if not odd and q >= 2:
-                cell_tanh(GT * (q - 2), GT)
-                store(oc_v, cn_t, GT * (q - 2), GT)
-            add_proj(j, 1, 0)
-            if more:
-                project(j + 1, 1, 0)
-            if len(by_pe) == 1:
-                add_bias(jb, 1, 0, 1)
-            add_proj(j, 1, 1)
-            if more:
-                project(j + 1, 1, 1)
-            if j == 0:
-                quantise(1, 0, GT)
-            if odd and 2 <= q <= 5:
-                hidden(GT * (q - 2), GT)
-                store(oh_v, hn_t, GT * (q - 2), GT)
-            if j == NPAIR - 2:
-                hidden(GT * 4, GT)
-                store(oh_v, hn_t, GT * 4, GT)
-            if odd and q + 2 < NG:
-                quantise(q + 2, 0, GT)
+        for j in range(1, NPAIR):
+            if j > 3:
+                for a in range(2):
+                    at(j - LTR + 0.05 + 0.1 * a, transposes, j, a)
+                    at(j - LTR + 0.1 + 0.2 * a, regroup, j, a)
+                if j % 2 == 0:
+                    at(j - LQ, quantise, 2 * j, 4)
+            tb = j - LB
+            if j not in GP and j < 4:
+                for i in range(2):
+                    at(-7.75 if j == 1 else -4 + j, add_bias, V, j, i, 0, 2)
+            elif j not in GP:
+                if j in PB:
+                    for a in range(2):
+                        at(tb + 0.1 + 0.3 * a, bias_matmul, j, a, 0)
+                        at(tb + 0.15 + 0.3 * a, bias_copy, j, a, 0)
+                else:
+                    at(tb + 0.26, add_bias, V, j, 0, 0, 2)
+                pe = [0, 1] if j in PE0 else [1]
+                va = [a for a in range(2) if a not in pe]
+                if va:
+                    at(tb + 0.6, add_bias, V, j, 1, va[0], len(va))
+                for a in pe:
+                    at(tb + 0.2 + 0.3 * a, bias_matmul, j, a)
+                    at(tb + 0.25 + 0.3 * a, bias_copy, j, a)
+            for a in range(2):
+                for nh in range(2):
+                    t = j + 0.5 * a + 0.25 * nh
+                    at(t - 0.98, project, j, a, nh)
+                    at(t, add_proj, j, a, nh)
+        t0 = 0
+        for u, nt in enumerate(UNITS):
+            for t in range(t0, t0 + nt):
+                w = 0.5 * t + 0.51
+                at(w, act, t, 1, 0, 512, ACT.Sigmoid)
+                at(w + 0.01, act, t, 1, 512, 768, ACT.Tanh)
+                at(w + 0.02, act, t, 1, 768, 1024, ACT.Sigmoid)
+            end = 0.5 * (t0 + nt)
+            small = nt < 4
+            eng = V if ENG[u] == "V" else G
+            dl = TD[u - len(UNITS)] if u - len(UNITS) in TD else 0.0
+            w = end + dl + (TLC if small else LC)
+            at(w, cell_f, eng, t0, nt)
+            at(w, cell_i, eng, t0, nt)
+            at(w + 0.02, cell_add, eng, t0, nt)
+            w = end + dl + (TLT if small else LT)
+            at(w, cell_tanh, t0, nt)
+            at(w + 0.01, store, oc_v, cn_t, t0, nt)
+            w = end + dl + (TLH if small else LH)
+            at(w, hidden, V, t0, nt)
+            at(w + 0.01, store, oh_v, hn_t, t0, nt)
+            t0 += nt
 
-        cell_state(GT * 6, GT, nc.vector)
-        activate(NT - 1)
-        cell_tanh(GT * 6, GT)
-        store(oc_v, cn_t, GT * 6, GT)
-        hidden(GT * 5, GT)
-        store(oh_v, hn_t, GT * 5, GT)
-        cell_state(NT - 4, 2, nc.vector)
-        cell_tanh(NT - 4, 2)
-        store(oc_v, cn_t, NT - 4, 2)
-        hidden(GT * 6, GT)
-        store(oh_v, hn_t, GT * 6, GT)
-        cell_state(NT - 2, 2, nc.vector)
-        cell_tanh(NT - 2, 2)
-        store(oc_v, cn_t, NT - 2, 2)
-        hidden(NT - 4, 2)
-        store(oh_v, hn_t, NT - 4, 2)
-        hidden(NT - 2, 2)
-        store(oh_v, hn_t, NT - 2, 2)
+        for when, k, fn, args in sorted(plan, key=lambda e: e[:2]):
+            fn(*args)

@@ -22,11 +22,11 @@ NT = B // P
 NPAIR = NT // 2
 HALF = 512
 
-GP = (1, 2)
+GP = ()
 PE0 = (5, 7, 9, 11, 13)
 UNITS = (4, 4, 4, 4, 4, 4, 4, 2, 1, 1)
-ENG = "GGGGGGGVVV"
-ORDER = "r0 h0 w0 w1 w2 w3 r1 h1 r2 h2 r3 h3 c0 c1"
+ENG = "GGGGGGVVVV"
+ORDER = "r0 h0 r1 w0 w1 w2 w3 h1 r2 h2 c0 r3 h3 c1"
 WV = (7,)
 PB = (14, 15)
 PRR = 4.9

@@ -22,26 +22,18 @@ NT = B // P
 NPAIR = NT // 2
 HALF = 512
 
-GP = ()
-PE0 = (5, 7, 9, 11, 13)
-UNITS = (4, 4, 4, 4, 4, 4, 4, 2, 1, 1)
-ENG = "GGGGGGVVVV"
-ORDER = "r0 h0 r1 w0 w1 w2 w3 h1 r2 h2 c0 r3 h3 c1"
 WV = (7,)
-PB = (14, 15)
-PRR = 4.9
-PRH = 5.8
-HT = 0.9
-TD = {-3: 1.0, -2: 0.5}
-LC = 0.4
-LT = 3.2
-LH = 4.27
-TLC = 0.5
-TLT = 1.2
-TLH = 1.7
-LQ = 1.72
-LTR = 3.9
-LB = 2.0
+GP = (2,)
+ORDER = "r0 h0 w0 w1 w2 w3 r1 h1 r2 h2 r3 h3 c0 c1 h4 h5"
+XB = 6
+PE2 = (5, 7, 9, 11, 13, 14, 15)
+RUN = 1
+H1 = 0
+B1 = 3
+A0 = 1
+R0 = 3
+CG = 7
+TPOS = 3
 
 
 def tile_yourlstm_pc_t_kernel(tc, h_below, gates_rec, c, w_ih, b_ih, b_hh, out_0, out_1):
@@ -71,21 +63,21 @@ def tile_yourlstm_pc_t_kernel(tc, h_below, gates_rec, c, w_ih, b_ih, b_hh, out_0
             nc.sync.dma_start(out=h_t[j][:], in_=h_v[:, j * 2 * K:(j + 1) * 2 * K])
 
         def load_c(q):
-            c_t[q] = loads.tile([P, 4 * H], BF16, tag="c", bufs=3, name="c_sb")
+            c_t[q] = loads.tile([P, 4 * H], BF16, tag="c", bufs=4, name="c_sb")
             nc.sync.dma_start(out=c_t[q][:], in_=c_v[:, q * 4 * H:(q + 1) * 4 * H])
 
         w_t, wq_t = {}, {}
 
         def load_w(i):
             if 0 not in w_t:
-                w_t[0] = work.tile([P, 8 * K], BF16, tag="x", bufs=5, name="w_sb", align_bytes=64)
+                w_t[0] = work.tile([P, 8 * K], BF16, tag="x", bufs=XB, name="w_sb", align_bytes=64)
             dst = w_t[0][:].rearrange("p (a k) -> p a k", a=8)
             nc.sync.dma_start(out=dst[:, 2 * i:2 * i + 2, :], in_=w_v[:, 2 * i:2 * i + 2, :])
 
         def x3(t):
             q = t // 4
             if q not in x_t:
-                x_t[q] = work.tile([P, 4 * N], F32, tag="x", bufs=5, name="x_sb", align_bytes=64)
+                x_t[q] = work.tile([P, 4 * N], F32, tag="x", bufs=XB, name="x_sb", align_bytes=64)
             return x_t[q][:].rearrange("p (a n) -> p a n", a=4)
 
         ident = const.tile([P, P], F32, name="ident")
@@ -167,7 +159,7 @@ def tile_yourlstm_pc_t_kernel(tc, h_below, gates_rec, c, w_ih, b_ih, b_hh, out_0
         def w_regroup(a, eng):
             half = a // 4
             if 0 not in wq_t:
-                wq_t[0] = work.tile([P, 8 * K], BF16, tag="x", bufs=5, name="wq", align_bytes=64)
+                wq_t[0] = work.tile([P, 8 * K], BF16, tag="x", bufs=XB, name="wq", align_bytes=64)
             dst = wq_t[0][:, half * 4 * K:(half + 1) * 4 * K].bitcast(F32).rearrange("p (g n u) -> p g n u", g=2, u=2)[:, :, P * (a % 4):P * (a % 4 + 1), :]
             src = wtp_t[a][:].rearrange("p (g u r) -> p g r u", g=2, u=2)
             if eng == "V":
@@ -237,104 +229,179 @@ def tile_yourlstm_pc_t_kernel(tc, h_below, gates_rec, c, w_ih, b_ih, b_hh, out_0
             lo = (t0 % 4) * H
             nc.sync.dma_start(out=dram[:, t0 * H:(t0 + nt) * H], in_=tiles[t0 // 4][:, lo:lo + nt * H])
 
-        plan = []
-
-        def at(when, fn, *args):
-            plan.append((when, len(plan), fn, args))
-
-
-        for k, e in enumerate(ORDER.split()):
-            at(-9 + 0.01 * k, {"h": load_h, "r": load_rec, "w": load_w, "c": load_c}[e[0]], int(e[1:]))
-        for j in range(4, NPAIR):
-            at(j - PRR, load_rec, j)
-            at(j - PRH, load_h, j)
-            if j % 2 == 0:
-                at(j - 4.7, load_c, j // 2)
-
         V, G = nc.vector, nc.gpsimd
-        for i in range(2):
-            at(-8, bias_rows, i)
-            at(-8, bias_out, i)
-        for a in range(2):
-            at(-7.9, transposes, 0, a)
-            at(-7.9, regroup, 0, a)
-        for i in range(2):
-            at(-7.8, add_bias, V, 0, i, 0, 2)
-        at(-7.7, quantise, 0, 2)
-        for a in range(8):
-            at(-7 + 0.25 * a, w_transposes, a)
-            at(-6.9 + 0.25 * a, w_regroup, a, "V" if a in WV else "S")
-        at(-6.1, w_quantise, 0)
-        for a in range(2):
-            at(-4.35, project, 0, a, 0)
-            at(-3.7, add_proj, 0, a, 0)
-        at(-5, w_quantise, 1)
-        for a in range(2):
-            at(-2.7, project, 0, a, 1)
-            at(0.5 * a, add_proj, 0, a, 1)
-        for p in (1, 2, 3):
-            for a in range(2):
-                at(-3.0 + HT * (p - 1), transposes, p, a)
-                at(-2.9 + HT * (p - 1), regroup, p, a)
-        at(-2.8, quantise, 2, 2)
-        at(0.1, quantise, 4, 4)
-        for j in GP:
-            for i in range(2):
-                for a in range(2):
-                    at(-7 + 0.1 * j, add_bias, G, j, i, a, 1, True)
 
-        for j in range(1, NPAIR):
-            if j > 3:
-                for a in range(2):
-                    at(j - LTR + 0.05 + 0.1 * a, transposes, j, a)
-                    at(j - LTR + 0.1 + 0.2 * a, regroup, j, a)
-                if j % 2 == 0:
-                    at(j - LQ, quantise, 2 * j, 4)
-            tb = j - LB
-            if j not in GP and j < 4:
+        def cells(eng, t0, nt):
+            cell_f(eng, t0, nt)
+            cell_i(eng, t0, nt)
+            cell_add(eng, t0, nt)
+
+        def tanh_c(t0, nt):
+            cell_tanh(t0, nt)
+            store(oc_v, cn_t, t0, nt)
+
+        def out_h(t0, nt):
+            hidden(V, t0, nt)
+            store(oh_v, hn_t, t0, nt)
+
+        def load(what):
+            {"h": load_h, "r": load_rec, "w": load_w, "c": load_c}[what[0]](int(what[1:]))
+
+        def two(fn, j):
+            for a in range(2):
+                fn(j, a)
+
+        for what in ORDER.split():
+            load(what)
+
+        def bias_all(j):
+            if j in GP:
                 for i in range(2):
-                    at(-7.75 if j == 1 else -4 + j, add_bias, V, j, i, 0, 2)
-            elif j not in GP:
-                if j in PB:
                     for a in range(2):
-                        at(tb + 0.1 + 0.3 * a, bias_matmul, j, a, 0)
-                        at(tb + 0.15 + 0.3 * a, bias_copy, j, a, 0)
-                else:
-                    at(tb + 0.26, add_bias, V, j, 0, 0, 2)
-                pe = [0, 1] if j in PE0 else [1]
-                va = [a for a in range(2) if a not in pe]
-                if va:
-                    at(tb + 0.6, add_bias, V, j, 1, va[0], len(va))
-                for a in pe:
-                    at(tb + 0.2 + 0.3 * a, bias_matmul, j, a)
-                    at(tb + 0.25 + 0.3 * a, bias_copy, j, a)
-            for a in range(2):
-                for nh in range(2):
-                    t = j + 0.5 * a + 0.25 * nh
-                    at(t - 0.98, project, j, a, nh)
-                    at(t, add_proj, j, a, nh)
-        t0 = 0
-        for u, nt in enumerate(UNITS):
-            for t in range(t0, t0 + nt):
-                w = 0.5 * t + 0.51
-                at(w, act, t, 1, 0, 512, ACT.Sigmoid)
-                at(w + 0.01, act, t, 1, 512, 768, ACT.Tanh)
-                at(w + 0.02, act, t, 1, 768, 1024, ACT.Sigmoid)
-            end = 0.5 * (t0 + nt)
-            small = nt < 4
-            eng = V if ENG[u] == "V" else G
-            dl = TD[u - len(UNITS)] if u - len(UNITS) in TD else 0.0
-            w = end + dl + (TLC if small else LC)
-            at(w, cell_f, eng, t0, nt)
-            at(w, cell_i, eng, t0, nt)
-            at(w + 0.02, cell_add, eng, t0, nt)
-            w = end + dl + (TLT if small else LT)
-            at(w, cell_tanh, t0, nt)
-            at(w + 0.01, store, oc_v, cn_t, t0, nt)
-            w = end + dl + (TLH if small else LH)
-            at(w, hidden, V, t0, nt)
-            at(w + 0.01, store, oh_v, hn_t, t0, nt)
-            t0 += nt
+                        add_bias(G, j, i, a, 1, True)
+            else:
+                for i in range(2):
+                    add_bias(V, j, i, 0, 2)
 
-        for when, k, fn, args in sorted(plan, key=lambda e: e[:2]):
-            fn(*args)
+        def w_block(a):
+            w_transposes(a)
+            w_regroup(a, "V" if a in WV else "S")
+
+        for i in range(2):
+            bias_rows(i)
+            bias_out(i)
+        two(transposes, 0)
+        two(regroup, 0)
+        bias_all(0)
+        if H1 == 0:
+            quantise(0, 2)
+        if H1 == 1:
+            two(transposes, 1)
+            two(regroup, 1)
+        if B1 == 0:
+            bias_all(1)
+        if H1 == 1:
+            quantise(0, 4)
+        for a in range(4):
+            w_block(a)
+        w_quantise(0)
+        if B1 == 1:
+            bias_all(1)
+        for a in range(4, 8):
+            w_block(a)
+        if B1 == 2:
+            bias_all(1)
+        for a in range(2):
+            project(0, a, 0)
+        if A0 == 0:
+            add_proj(0, 0, 0)
+            add_proj(0, 1, 0)
+        w_quantise(1)
+        if A0 == 1:
+            add_proj(0, 0, 0)
+            add_proj(0, 1, 0)
+        if B1 == 3:
+            bias_all(1)
+        if H1 == 0:
+            two(transposes, 1)
+            two(regroup, 1)
+        for a in range(2):
+            project(0, a, 1)
+        if H1 == 0:
+            quantise(2, 2)
+        for p in range(2, 4):
+            two(transposes, p)
+            two(regroup, p)
+        if 2 in GP:
+            bias_all(2)
+        two(transposes, 4)
+
+        for j in range(NPAIR):
+            q = j // 2
+            even = j % 2 == 0
+            more = j + 1 < NPAIR
+            jb = j + 2
+            bias = jb < NPAIR and jb not in GP
+            pe = ([0, 1] if jb in PE2 else [1]) if bias and jb > 3 else []
+            if j + 4 < NPAIR:
+                load_rec(j + 4)
+            if j + 6 < NPAIR:
+                load_h(j + 6)
+            if even and q + 2 < NPAIR // 2:
+                load_c(q + 2)
+
+            if j + 4 < NPAIR:
+                two(regroup, j + 4)
+            if j > 0:
+                add_proj(j, 0, 0)
+            if more:
+                project(j + 1, 0, 0)
+            for a in pe:
+                bias_matmul(jb, a)
+            if j > 0:
+                act(2 * j - 2, 2, 0, 512, ACT.Sigmoid)
+            if pe:
+                bias_copy(jb, pe[0])
+            if j > 0:
+                act(2 * j - 2, 2, 512, 768, ACT.Tanh)
+            if len(pe) > 1:
+                bias_copy(jb, pe[1])
+            if j > 0:
+                act(2 * j - 2, 2, 768, 1024, ACT.Sigmoid)
+            if even and 1 <= q <= CG:
+                cells(G, 4 * q - 4, 4)
+            def run():
+                if even and q >= 3:
+                    out_h(4 * (q - 3), 4)
+                if j == 0:
+                    quantise(4, 4)
+                elif even and q + 1 < NPAIR // 2:
+                    quantise(4 * q + 4, 4)
+            rn = R0 if j == 0 else RUN
+            if rn == 0:
+                run()
+            if bias:
+                add_bias(V, jb, 0, 0, 2)
+            if rn == 1:
+                run()
+            add_proj(j, 0, 1)
+            if more:
+                project(j + 1, 0, 1)
+            if rn == 2:
+                run()
+            if j > 0:
+                add_proj(j, 1, 0)
+            if more:
+                project(j + 1, 1, 0)
+            if bias and len(pe) < 2:
+                add_bias(V, jb, 1, 0, 1 if pe else 2)
+            if rn == 3:
+                run()
+            add_proj(j, 1, 1)
+            if TPOS == 3 and j + 5 < NPAIR:
+                two(transposes, j + 5)
+            if more:
+                project(j + 1, 1, 1)
+            if TPOS == 4 and j + 5 < NPAIR:
+                two(transposes, j + 5)
+            if even and q >= 2:
+                tanh_c(4 * (q - 2), 4)
+
+        for t in (30, 31):
+            act(t, 1, 0, 512, ACT.Sigmoid)
+            act(t, 1, 512, 768, ACT.Tanh)
+            act(t, 1, 768, 1024, ACT.Sigmoid)
+        if CG == 6:
+            cells(V, 24, 4)
+        cells(V, 28, 2)
+        out_h(20, 4)
+        tanh_c(24, 4)
+        tanh_c(28, 2)
+        cells(V, 30, 1)
+        tanh_c(30, 1)
+        out_h(24, 4)
+        cells(V, 31, 1)
+        tanh_c(31, 1)
+        out_h(28, 2)
+        out_h(30, 1)
+        out_h(31, 1)

@@ -23,13 +23,15 @@ NPAIR = NT // 2
 HALF = 512
 
 WV = (7,)
-GP = (2,)
-ORDER = "r0 h0 w0 w1 w2 w3 r1 h1 r2 h2 r3 h3 c0 c1 h4 h5"
+GP = (1,)
+ORDER = "r0 h0 w0 w1 w2 w3 h1 r1 h2 r2 h3 r3 c0 c1 h4 h5"
 XB = 6
-PE2 = (5, 7, 9, 11, 13, 14, 15)
+PE2 = (4, 6, 8, 10, 12, 13, 14, 15)
+FV = 2
+RO = "fhq"
 RUN = 1
 H1 = 0
-B1 = 3
+B1 = 1
 A0 = 1
 R0 = 3
 CG = 7
@@ -349,14 +351,16 @@ def tile_yourlstm_pc_t_kernel(tc, h_below, gates_rec, c, w_ih, b_ih, b_hh, out_0
             if j > 0:
                 act(2 * j - 2, 2, 768, 1024, ACT.Sigmoid)
             if even and 1 <= q <= CG:
-                cells(G, 4 * q - 4, 4)
+                cell_f(G, 4 * q - 4 + FV, 4 - FV)
+                cell_i(G, 4 * q - 4, 4)
             def run():
-                if even and q >= 3:
-                    out_h(4 * (q - 3), 4)
-                if j == 0:
-                    quantise(4, 4)
-                elif even and q + 1 < NPAIR // 2:
-                    quantise(4 * q + 4, 4)
+                for what in RO:
+                    if what == "h" and even and q >= 3:
+                        out_h(4 * (q - 3), 4)
+                    if what == "f" and FV and even and 1 <= q <= CG:
+                        cell_f(V, 4 * q - 4, FV)
+                    if what == "q" and even and q + 1 < NPAIR // 2:
+                        quantise(4 * q + 4, 4)
             rn = R0 if j == 0 else RUN
             if rn == 0:
                 run()
@@ -384,6 +388,10 @@ def tile_yourlstm_pc_t_kernel(tc, h_below, gates_rec, c, w_ih, b_ih, b_hh, out_0
                 project(j + 1, 1, 1)
             if TPOS == 4 and j + 5 < NPAIR:
                 two(transposes, j + 5)
+            if j in (13, 15) and q > CG:
+                cells(V, 4 * q - 4, 4)
+            if even and 1 <= q <= CG:
+                cell_add(G, 4 * q - 4, 4)
             if even and q >= 2:
                 tanh_c(4 * (q - 2), 4)
 
@@ -391,8 +399,6 @@ def tile_yourlstm_pc_t_kernel(tc, h_below, gates_rec, c, w_ih, b_ih, b_hh, out_0
             act(t, 1, 0, 512, ACT.Sigmoid)
             act(t, 1, 512, 768, ACT.Tanh)
             act(t, 1, 768, 1024, ACT.Sigmoid)
-        if CG == 6:
-            cells(V, 24, 4)
         cells(V, 28, 2)
         out_h(20, 4)
         tanh_c(24, 4)

@@ -24,16 +24,20 @@ HALF = 512
 
 WV = (7,)
 GP = (1,)
-ORDER = "r0 h0 w0 w1 w2 w3 h1 r1 h2 r2 h3 r3 c0 c1 h4 h5"
+ORDER = "r0 h0 w0 w1 w2 w3 r1 h1 h2 h3 r2 c0 h4 r3 c1"
 XB = 6
-PE2 = (4, 6, 8, 10, 12, 13, 14, 15)
-FV = 2
+R = 3
+PN = (0, 0, 1, 1, 2, 1, 2, 1, 2, 1, 2, 1, 2, 2, 2, 2)
+FV = 1
+F6 = 1
+A6 = "V"
+TAIL = "h204 a244 t244 c282 t282 c301 t301 h244 c311 t311 h282 h301 h311"
 RO = "fhq"
 RUN = 1
-H1 = 0
-B1 = 1
-A0 = 1
+HEAD = "R0 R1 O0 O1 T0 g0 B0 Q2 w0 k0 w1 k1 w2 k2 w3 k3 W0 B1 w4 k4 w5 k5 w6 k6 w7 k7 M0 M10 W1 A0 A10 T1 g1 M1 M11 Q22 T2 g2 T3"
+V_G = "S"
 R0 = 3
+R14 = 3
 CG = 7
 TPOS = 3
 
@@ -137,12 +141,16 @@ def tile_yourlstm_pc_t_kernel(tc, h_below, gates_rec, c, w_ih, b_ih, b_hh, out_0
             tp_t[(j, a)] = psum.tile([P, HALF], F32, tag="tp", bufs=2, name="tp")
             four_transposes(tp_t[(j, a)], h_t[j][:].bitcast(F32)[:, 512 * a:512 * (a + 1)])
 
-        def regroup(j, a):
+        def regroup(j, a, eng="S"):
             q = j // 2
             if q not in gq_t:
                 gq_t[q] = work.tile([P, 4 * K], BF16, tag="gq", bufs=3, name="gq", align_bytes=64)
             gq_w = gq_t[q][:].bitcast(F32).rearrange("p (t g r u) -> p t g r u", t=4, g=2, u=2)
-            nc.scalar.copy(out=gq_w[:, (2 * j) % 4 + a], in_=tp_t[(j, a)][:].rearrange("p (g u r) -> p g r u", g=2, u=2))
+            src = tp_t[(j, a)][:].rearrange("p (g u r) -> p g r u", g=2, u=2)
+            if eng == "V":
+                nc.vector.tensor_copy(out=gq_w[:, (2 * j) % 4 + a], in_=src)
+            else:
+                nc.scalar.copy(out=gq_w[:, (2 * j) % 4 + a], in_=src)
 
         def quantise(t0, nt):
             q = t0 // 4
@@ -269,54 +277,31 @@ def tile_yourlstm_pc_t_kernel(tc, h_below, gates_rec, c, w_ih, b_ih, b_hh, out_0
             w_transposes(a)
             w_regroup(a, "V" if a in WV else "S")
 
-        for i in range(2):
-            bias_rows(i)
-            bias_out(i)
-        two(transposes, 0)
-        two(regroup, 0)
-        bias_all(0)
-        if H1 == 0:
-            quantise(0, 2)
-        if H1 == 1:
-            two(transposes, 1)
-            two(regroup, 1)
-        if B1 == 0:
-            bias_all(1)
-        if H1 == 1:
-            quantise(0, 4)
-        for a in range(4):
-            w_block(a)
-        w_quantise(0)
-        if B1 == 1:
-            bias_all(1)
-        for a in range(4, 8):
-            w_block(a)
-        if B1 == 2:
-            bias_all(1)
-        for a in range(2):
-            project(0, a, 0)
-        if A0 == 0:
-            add_proj(0, 0, 0)
-            add_proj(0, 1, 0)
-        w_quantise(1)
-        if A0 == 1:
-            add_proj(0, 0, 0)
-            add_proj(0, 1, 0)
-        if B1 == 3:
-            bias_all(1)
-        if H1 == 0:
-            two(transposes, 1)
-            two(regroup, 1)
-        for a in range(2):
-            project(0, a, 1)
-        if H1 == 0:
-            quantise(2, 2)
-        for p in range(2, 4):
-            two(transposes, p)
-            two(regroup, p)
-        if 2 in GP:
-            bias_all(2)
-        two(transposes, 4)
+        for what in HEAD.split():
+            kind, n = what[0], int(what[1:] or 0)
+            if kind == "R":
+                bias_rows(n)
+            if kind == "O":
+                bias_out(n)
+            if kind == "T":
+                two(transposes, n)
+            if kind == "g":
+                for a in range(2):
+                    regroup(n, a, V_G if n == 0 else "S")
+            if kind == "B":
+                bias_all(n)
+            if kind == "Q":
+                quantise(n // 10, n % 10)
+            if kind == "w":
+                w_transposes(n)
+            if kind == "k":
+                w_regroup(n, "V" if n in WV else "S")
+            if kind == "W":
+                w_quantise(n)
+            if kind == "M":
+                project(0, n // 10, n % 10)
+            if kind == "A":
+                add_proj(0, n // 10, n % 10)
 
         for j in range(NPAIR):
             q = j // 2
@@ -324,16 +309,16 @@ def tile_yourlstm_pc_t_kernel(tc, h_below, gates_rec, c, w_ih, b_ih, b_hh, out_0
             more = j + 1 < NPAIR
             jb = j + 2
             bias = jb < NPAIR and jb not in GP
-            pe = ([0, 1] if jb in PE2 else [1]) if bias and jb > 3 else []
+            pe = [[], [1], [0, 1]][PN[jb]] if bias else []
             if j + 4 < NPAIR:
                 load_rec(j + 4)
-            if j + 6 < NPAIR:
-                load_h(j + 6)
+            if j + R + 2 < NPAIR:
+                load_h(j + R + 2)
             if even and q + 2 < NPAIR // 2:
                 load_c(q + 2)
 
-            if j + 4 < NPAIR:
-                two(regroup, j + 4)
+            if j + R < NPAIR:
+                two(regroup, j + R)
             if j > 0:
                 add_proj(j, 0, 0)
             if more:
@@ -351,17 +336,19 @@ def tile_yourlstm_pc_t_kernel(tc, h_below, gates_rec, c, w_ih, b_ih, b_hh, out_0
             if j > 0:
                 act(2 * j - 2, 2, 768, 1024, ACT.Sigmoid)
             if even and 1 <= q <= CG:
-                cell_f(G, 4 * q - 4 + FV, 4 - FV)
+                fv = F6 if q == 7 else FV
+                if fv < 4:
+                    cell_f(G, 4 * q - 4 + fv, 4 - fv)
                 cell_i(G, 4 * q - 4, 4)
             def run():
                 for what in RO:
                     if what == "h" and even and q >= 3:
                         out_h(4 * (q - 3), 4)
-                    if what == "f" and FV and even and 1 <= q <= CG:
-                        cell_f(V, 4 * q - 4, FV)
+                    if what == "f" and even and 1 <= q <= CG and fv:
+                        cell_f(V, 4 * q - 4, fv)
                     if what == "q" and even and q + 1 < NPAIR // 2:
                         quantise(4 * q + 4, 4)
-            rn = R0 if j == 0 else RUN
+            rn = R0 if j == 0 else R14 if j == 14 else RUN
             if rn == 0:
                 run()
             if bias:
@@ -382,15 +369,15 @@ def tile_yourlstm_pc_t_kernel(tc, h_below, gates_rec, c, w_ih, b_ih, b_hh, out_0
             if rn == 3:
                 run()
             add_proj(j, 1, 1)
-            if TPOS == 3 and j + 5 < NPAIR:
-                two(transposes, j + 5)
+            if rn == 4:
+                run()
+            if TPOS == 3 and j + R + 1 < NPAIR:
+                two(transposes, j + R + 1)
             if more:
                 project(j + 1, 1, 1)
-            if TPOS == 4 and j + 5 < NPAIR:
-                two(transposes, j + 5)
-            if j in (13, 15) and q > CG:
-                cells(V, 4 * q - 4, 4)
-            if even and 1 <= q <= CG:
+            if TPOS == 4 and j + R + 1 < NPAIR:
+                two(transposes, j + R + 1)
+            if even and 1 <= q <= CG and not (q == 7 and A6 == "V"):
                 cell_add(G, 4 * q - 4, 4)
             if even and q >= 2:
                 tanh_c(4 * (q - 2), 4)
@@ -399,15 +386,17 @@ def tile_yourlstm_pc_t_kernel(tc, h_below, gates_rec, c, w_ih, b_ih, b_hh, out_0
             act(t, 1, 0, 512, ACT.Sigmoid)
             act(t, 1, 512, 768, ACT.Tanh)
             act(t, 1, 768, 1024, ACT.Sigmoid)
-        cells(V, 28, 2)
-        out_h(20, 4)
-        tanh_c(24, 4)
-        tanh_c(28, 2)
-        cells(V, 30, 1)
-        tanh_c(30, 1)
-        out_h(24, 4)
-        cells(V, 31, 1)
-        tanh_c(31, 1)
-        out_h(28, 2)
-        out_h(30, 1)
-        out_h(31, 1)
+        for what in TAIL.split():
+            kind, t0, nt = what[0], int(what[1:3]), int(what[3:])
+            if kind == "a":
+                cell_add(V, t0, nt)
+            if kind == "c":
+                cells(V, t0, nt)
+            if kind == "f":
+                cell_f(V, t0, nt)
+            if kind == "i":
+                cell_i(V, t0, nt)
+            if kind == "t":
+                tanh_c(t0, nt)
+            if kind == "h":
+                out_h(t0, nt)

@@ -24,20 +24,23 @@ HALF = 512
 
 WV = (7,)
 GP = (1,)
-ORDER = "r0 h0 w0 w1 w2 w3 r1 h1 h2 h3 r2 c0 h4 r3 c1"
+ORDER = "r0 h0 w0 w1 w2 w3 r1 h1 r2 h2 h3 c0 h4 r3 c1"
 XB = 6
 R = 3
-PN = (0, 0, 1, 1, 2, 1, 2, 1, 2, 1, 2, 1, 2, 2, 2, 2)
+PN = (0, 0, 1, 1, 2, 1, 2, 1, 2, 1, 2, 1, 2, 1, 2, 1)
 FV = 1
-F6 = 1
+F6 = 4
 A6 = "V"
 TAIL = "h204 a244 t244 c282 t282 c301 t301 h244 c311 t311 h282 h301 h311"
 RO = "fhq"
-RUN = 1
+RUN = 2
 HEAD = "R0 R1 O0 O1 T0 g0 B0 Q2 w0 k0 w1 k1 w2 k2 w3 k3 W0 B1 w4 k4 w5 k5 w6 k6 w7 k7 M0 M10 W1 A0 A10 T1 g1 M1 M11 Q22 T2 g2 T3"
 V_G = "S"
+SO = "S01T"
+R1 = 3
+F5 = 1
 R0 = 3
-R14 = 3
+R14 = 4
 CG = 7
 TPOS = 3
 
@@ -86,6 +89,14 @@ def tile_yourlstm_pc_t_kernel(tc, h_below, gates_rec, c, w_ih, b_ih, b_hh, out_0
                 x_t[q] = work.tile([P, 4 * N], F32, tag="x", bufs=XB, name="x_sb", align_bytes=64)
             return x_t[q][:].rearrange("p (a n) -> p a n", a=4)
 
+        def half(t0, nt, i):
+            x = x_blocks(t0)[:, t0 % 4:t0 % 4 + nt]
+            return x[:, :, 1:3, :] if i == 0 else x[:, :, 0:4:3, :]
+
+        def x_blocks(t0):
+            x3(t0)
+            return x_t[t0 // 4][:].rearrange("p (a b n) -> p a b n", a=4, b=4)
+
         ident = const.tile([P, P], F32, name="ident")
         make_identity(nc, ident[:])
         identb = const.tile([P, P], BF16, name="identb")
@@ -113,10 +124,10 @@ def tile_yourlstm_pc_t_kernel(tc, h_below, gates_rec, c, w_ih, b_ih, b_hh, out_0
         def add_bias(eng, j, i, a0, na, pool=False):
             r3 = r_t[j][:].rearrange("p (a n) -> p a n", a=2)
             s = slice(HALF * i, HALF * (i + 1))
-            row = (bias_sb[:, s] if pool else bias_ps[i][:]).unsqueeze(1).to_broadcast([P, na, HALF])
-            rec = r3[:, a0:a0 + na, s]
+            row = (bias_sb[:, s] if pool else bias_ps[i][:]).rearrange("p (b n) -> p b n", b=2).unsqueeze(1).to_broadcast([P, na, 2, 256])
+            rec = r3[:, a0:a0 + na, s].rearrange("p a (b n) -> p a b n", b=2)
             eng.tensor_tensor(
-                out=x3(2 * j)[:, (2 * j) % 4 + a0:(2 * j) % 4 + a0 + na, s],
+                out=half(2 * j + a0, na, i),
                 in0=rec if pool else row,
                 in1=row if pool else rec,
                 op=ALU.add,
@@ -130,7 +141,7 @@ def tile_yourlstm_pc_t_kernel(tc, h_below, gates_rec, c, w_ih, b_ih, b_hh, out_0
             nc.tensor.matmul(pre[:], lhsT=ones[:], rhs=brow[:, s], start=False, stop=True)
 
         def bias_copy(j, a, i=1):
-            nc.scalar.copy(out=x3(2 * j)[:, (2 * j) % 4 + a, HALF * i:HALF * (i + 1)], in_=pre_t[(j, a, i)][:])
+            nc.scalar.copy(out=half(2 * j + a, 1, i)[:, 0], in_=pre_t[(j, a, i)][:].rearrange("p (b n) -> p b n", b=2))
 
         def four_transposes(out, words):
             for jj in range(4):
@@ -198,8 +209,8 @@ def tile_yourlstm_pc_t_kernel(tc, h_below, gates_rec, c, w_ih, b_ih, b_hh, out_0
                 )
 
         def add_proj(j, a, nh):
-            dst = x3(2 * j)[:, (2 * j) % 4 + a, HALF * nh:HALF * (nh + 1)]
-            nc.vector.tensor_tensor(out=dst, in0=acc_t[(j, a, nh)][:], in1=dst, op=ALU.add)
+            dst = half(2 * j + a, 1, nh)[:, 0]
+            nc.vector.tensor_tensor(out=dst, in0=acc_t[(j, a, nh)][:].rearrange("p (b n) -> p b n", b=2), in1=dst, op=ALU.add)
 
         def sl(t0, nt):
             return slice(t0 % 4, t0 % 4 + nt)
@@ -215,25 +226,25 @@ def tile_yourlstm_pc_t_kernel(tc, h_below, gates_rec, c, w_ih, b_ih, b_hh, out_0
             return tiles[q][:].rearrange("p (a n) -> p a n", a=4)
 
         def cell_f(eng, t0, nt):
-            x = x3(t0)[:, sl(t0, nt), 256:512]
+            x = x3(t0)[:, sl(t0, nt), 512:768]
             c3 = c_t[t0 // 4][:].rearrange("p (a n) -> p a n", a=4)
             eng.tensor_tensor(out=x, in0=x, in1=c3[:, sl(t0, nt), :], op=ALU.mult)
 
         def cell_i(eng, t0, nt):
             x = x3(t0)[:, sl(t0, nt), :]
-            eng.tensor_tensor(out=x[:, :, 0:256], in0=x[:, :, 0:256], in1=x[:, :, 512:768], op=ALU.mult)
+            eng.tensor_tensor(out=x[:, :, 256:512], in0=x[:, :, 256:512], in1=x[:, :, 0:256], op=ALU.mult)
 
         def cell_add(eng, t0, nt):
             x = x3(t0)[:, sl(t0, nt), :]
-            eng.tensor_tensor(out=out3(cn_t, t0, "cn")[:, sl(t0, nt), :], in0=x[:, :, 0:256], in1=x[:, :, 256:512], op=ALU.add)
+            eng.tensor_tensor(out=out3(cn_t, t0, "cn")[:, sl(t0, nt), :], in0=x[:, :, 256:512], in1=x[:, :, 512:768], op=ALU.add)
 
         def cell_tanh(t0, nt):
-            x = x3(t0)[:, sl(t0, nt), 512:768]
+            x = x3(t0)[:, sl(t0, nt), 0:256]
             nc.scalar.activation(out=x, in_=out3(cn_t, t0, "cn")[:, sl(t0, nt), :], func=ACT.Tanh)
 
         def hidden(eng, t0, nt):
             x = x3(t0)[:, sl(t0, nt), :]
-            eng.tensor_tensor(out=out3(hn_t, t0, "hn")[:, sl(t0, nt), :], in0=x[:, :, 768:1024], in1=x[:, :, 512:768], op=ALU.mult)
+            eng.tensor_tensor(out=out3(hn_t, t0, "hn")[:, sl(t0, nt), :], in0=x[:, :, 768:1024], in1=x[:, :, 0:256], op=ALU.mult)
 
         def store(dram, tiles, t0, nt):
             lo = (t0 % 4) * H
@@ -325,18 +336,17 @@ def tile_yourlstm_pc_t_kernel(tc, h_below, gates_rec, c, w_ih, b_ih, b_hh, out_0
                 project(j + 1, 0, 0)
             for a in pe:
                 bias_matmul(jb, a)
-            if j > 0:
-                act(2 * j - 2, 2, 0, 512, ACT.Sigmoid)
-            if pe:
-                bias_copy(jb, pe[0])
-            if j > 0:
-                act(2 * j - 2, 2, 512, 768, ACT.Tanh)
-            if len(pe) > 1:
-                bias_copy(jb, pe[1])
-            if j > 0:
-                act(2 * j - 2, 2, 768, 1024, ACT.Sigmoid)
+            for what in SO:
+                if what == "T" and j > 0:
+                    act(2 * j - 2, 2, 0, 256, ACT.Tanh)
+                if what == "S" and j > 0:
+                    act(2 * j - 2, 2, 256, 1024, ACT.Sigmoid)
+                if what == "0" and pe:
+                    bias_copy(jb, pe[0])
+                if what == "1" and len(pe) > 1:
+                    bias_copy(jb, pe[1])
             if even and 1 <= q <= CG:
-                fv = F6 if q == 7 else FV
+                fv = F6 if q == 7 else F5 if q == 6 else FV
                 if fv < 4:
                     cell_f(G, 4 * q - 4 + fv, 4 - fv)
                 cell_i(G, 4 * q - 4, 4)
@@ -346,9 +356,11 @@ def tile_yourlstm_pc_t_kernel(tc, h_below, gates_rec, c, w_ih, b_ih, b_hh, out_0
                         out_h(4 * (q - 3), 4)
                     if what == "f" and even and 1 <= q <= CG and fv:
                         cell_f(V, 4 * q - 4, fv)
-                    if what == "q" and even and q + 1 < NPAIR // 2:
+                    if what == "q" and j < 2:
+                        quantise(4 + 2 * j, 2)
+                    elif what == "q" and even and q + 1 < NPAIR // 2:
                         quantise(4 * q + 4, 4)
-            rn = R0 if j == 0 else R14 if j == 14 else RUN
+            rn = (R0, R1)[j] if j < 2 else R14 if j == 14 else RUN
             if rn == 0:
                 run()
             if bias:
@@ -383,9 +395,8 @@ def tile_yourlstm_pc_t_kernel(tc, h_below, gates_rec, c, w_ih, b_ih, b_hh, out_0
                 tanh_c(4 * (q - 2), 4)
 
         for t in (30, 31):
-            act(t, 1, 0, 512, ACT.Sigmoid)
-            act(t, 1, 512, 768, ACT.Tanh)
-            act(t, 1, 768, 1024, ACT.Sigmoid)
+            act(t, 1, 0, 256, ACT.Tanh)
+            act(t, 1, 256, 1024, ACT.Sigmoid)
         for what in TAIL.split():
             kind, t0, nt = what[0], int(what[1:3]), int(what[3:])
             if kind == "a":

@@ -28,7 +28,7 @@ ORDER = "r0 h0 w0 w1 w2 w3 r1 h1 r2 h2 h3 c0 h4 r3 c1"
 XB = 6
 R = 3
 PN = (0, 0, 1, 1, 2, 1, 2, 1, 2, 1, 2, 1, 2, 1, 2, 1)
-FV = 1
+FV = 0
 F6 = 4
 A6 = "V"
 TAIL = "h204 a244 t244 c282 t282 c301 t301 h244 c311 t311 h282 h301 h311"
@@ -38,7 +38,7 @@ HEAD = "R0 R1 O0 O1 T0 g0 B0 Q2 w0 k0 w1 k1 w2 k2 w3 k3 W0 B1 w4 k4 w5 k5 w6 k6 
 V_G = "S"
 SO = "S01T"
 R1 = 3
-F5 = 1
+F5 = 0
 R0 = 3
 R14 = 4
 CG = 7

@@ -24,22 +24,23 @@ HALF = 512
 
 WV = (7,)
 GP = (1,)
-ORDER = "r0 h0 w0 w1 w2 w3 r1 h1 r2 h2 h3 c0 h4 r3 c1"
+ORDER = "r0 h0 w0 w1 w2 w3 h1 r1 h2 r2 h3 c0 h4 r3 c1"
 XB = 6
 R = 3
 PN = (0, 0, 1, 1, 2, 1, 2, 1, 2, 1, 2, 1, 2, 1, 2, 1)
-FV = 0
+TQ = 0
+FV = 1
 F6 = 4
 A6 = "V"
 TAIL = "h204 a244 t244 c282 t282 c301 t301 h244 c311 t311 h282 h301 h311"
 RO = "fhq"
-RUN = 2
+RUN = 3
 HEAD = "R0 R1 O0 O1 T0 g0 B0 Q2 w0 k0 w1 k1 w2 k2 w3 k3 W0 B1 w4 k4 w5 k5 w6 k6 w7 k7 M0 M10 W1 A0 A10 T1 g1 M1 M11 Q22 T2 g2 T3"
 V_G = "S"
 SO = "S01T"
 R1 = 3
-F5 = 0
-R0 = 3
+F5 = 1
+R0 = 2
 R14 = 4
 CG = 7
 TPOS = 3
@@ -337,8 +338,12 @@ def tile_yourlstm_pc_t_kernel(tc, h_below, gates_rec, c, w_ih, b_ih, b_hh, out_0
             for a in pe:
                 bias_matmul(jb, a)
             for what in SO:
-                if what == "T" and j > 0:
+                if what == "T" and j > 0 and not TQ:
                     act(2 * j - 2, 2, 0, 256, ACT.Tanh)
+                if what == "T" and even and j > 0 and TQ:
+                    act(2 * j - 4, 4, 0, 256, ACT.Tanh)
+                if what == "T" and j == 15 and TQ:
+                    act(28, 2, 0, 256, ACT.Tanh)
                 if what == "S" and j > 0:
                     act(2 * j - 2, 2, 256, 1024, ACT.Sigmoid)
                 if what == "0" and pe:

from contextlib import ExitStack

import concourse.mybir as mybir
from concourse.masks import make_identity

FLOPS = 2 * 4096 * 1024 * 1024

F32 = mybir.dt.float32
BF16 = mybir.dt.bfloat16
U32 = mybir.dt.uint32
U8 = mybir.dt.uint8
FP8X4 = mybir.dt.float8_e4m3fn_x4
ACT = mybir.ActivationFunctionType
ALU = mybir.AluOpType

P = 128
B = 4096
K = 1024
N = 1024
H = 256
NT = B // P
NPAIR = NT // 2
HALF = 512

WV = (7,)
GP = (1,)
ORDER = "r0 h0 w0 w1 w2 w3 h1 r1 h2 r2 h3 c0 h4 r3 c1"
XB = 6
R = 3
PN = (0, 0, 1, 1, 2, 1, 2, 1, 2, 1, 2, 1, 2, 1, 2, 1)
TQ = 0
FV = 1
F6 = 4
A6 = "V"
TAIL = "h204 a244 t244 c282 t282 c301 t301 h244 c311 t311 h282 h301 h311"
RO = "fhq"
RUN = 3
HEAD = "R0 R1 O0 O1 T0 g0 B0 Q2 w0 k0 w1 k1 w2 k2 w3 k3 W0 B1 w4 k4 w5 k5 w6 k6 w7 k7 M0 M10 W1 A0 A10 T1 g1 M1 M11 Q22 T2 g2 T3"
V_G = "S"
SO = "S01T"
R1 = 3
F5 = 1
R0 = 2
R14 = 4
CG = 7
TPOS = 3


def tile_yourlstm_pc_t_kernel(tc, h_below, gates_rec, c, w_ih, b_ih, b_hh, out_0, out_1):
    nc = tc.nc
    h_v = h_below.rearrange("(p t) k -> p (t k)", t=NT)
    r_v = gates_rec.rearrange("(p t) n -> p (t n)", t=NT)
    c_v = c.rearrange("(p t) n -> p (t n)", t=NT)
    oh_v = out_0.rearrange("(p t) n -> p (t n)", t=NT)
    oc_v = out_1.rearrange("(p t) n -> p (t n)", t=NT)
    w_v = w_ih.rearrange("(a p) k -> p a k", p=P)

    with ExitStack() as ctx:
        ctx.enter_context(tc.manual_schedule())
        const = ctx.enter_context(tc.tile_pool(name="const", bufs=1))
        loads = ctx.enter_context(tc.tile_pool(name="loads", bufs=5))
        work = ctx.enter_context(tc.tile_pool(name="work", bufs=3))
        psum = ctx.enter_context(tc.psum_pool(name="psum", bufs=1))

        h_t, r_t, c_t, x_t, cn_t, hn_t, tp_t, pre_t, gq_t, hc_t, hs_t, acc_t = [{} for i in range(12)]

        def load_rec(j):
            r_t[j] = loads.tile([P, 2 * N], BF16, tag="rec", name="rec_sb")
            nc.sync.dma_start(out=r_t[j][:], in_=r_v[:, j * 2 * N:(j + 1) * 2 * N])

        def load_h(j):
            h_t[j] = loads.tile([P, 2 * K], BF16, tag="h", name="h_sb")
            nc.sync.dma_start(out=h_t[j][:], in_=h_v[:, j * 2 * K:(j + 1) * 2 * K])

        def load_c(q):
            c_t[q] = loads.tile([P, 4 * H], BF16, tag="c", bufs=4, name="c_sb")
            nc.sync.dma_start(out=c_t[q][:], in_=c_v[:, q * 4 * H:(q + 1) * 4 * H])

        w_t, wq_t = {}, {}

        def load_w(i):
            if 0 not in w_t:
                w_t[0] = work.tile([P, 8 * K], BF16, tag="x", bufs=XB, name="w_sb", align_bytes=64)
            dst = w_t[0][:].rearrange("p (a k) -> p a k", a=8)
            nc.sync.dma_start(out=dst[:, 2 * i:2 * i + 2, :], in_=w_v[:, 2 * i:2 * i + 2, :])

        def x3(t):
            q = t // 4
            if q not in x_t:
                x_t[q] = work.tile([P, 4 * N], F32, tag="x", bufs=XB, name="x_sb", align_bytes=64)
            return x_t[q][:].rearrange("p (a n) -> p a n", a=4)

        def half(t0, nt, i):
            x = x_blocks(t0)[:, t0 % 4:t0 % 4 + nt]
            return x[:, :, 1:3, :] if i == 0 else x[:, :, 0:4:3, :]

        def x_blocks(t0):
            x3(t0)
            return x_t[t0 // 4][:].rearrange("p (a b n) -> p a b n", a=4, b=4)

        ident = const.tile([P, P], F32, name="ident")
        make_identity(nc, ident[:])
        identb = const.tile([P, P], BF16, name="identb")
        make_identity(nc, identb[:])
        ones = const.tile([P, P], BF16, name="ones")
        nc.vector.memset(ones[:], 1.0)
        brow = const.tile([P, N], BF16, name="brow")
        nc.vector.memset(brow[:], 0.0)
        nc.sync.dma_start(out=brow[0:1, :], in_=b_ih.rearrange("(o n) -> o n", o=1))
        nc.sync.dma_start(out=brow[1:2, :], in_=b_hh.rearrange("(o n) -> o n", o=1))
        warm = const.tile([P, 1], F32, name="warm")
        nc.vector.memset(warm[:], 0.0)
        nc.scalar.activation(out=warm[:], in_=warm[:], func=ACT.Sigmoid)
        wc = const.tile([P, 2 * N], U32, name="wc", align_bytes=64)
        ws = const.tile([P, 2 * N], U8, name="ws", align_bytes=64)
        bias_sb = const.tile([P, N], F32, name="bias_sb")
        bias_ps = [psum.tile([P, HALF], F32, name="bias%d" % i) for i in range(2)]

        def bias_rows(i):
            nc.tensor.matmul(bias_ps[i][:], lhsT=ones[:], rhs=brow[:, HALF * i:HALF * (i + 1)], start=True, stop=True)

        def bias_out(i):
            nc.scalar.copy(out=bias_sb[:, HALF * i:HALF * (i + 1)], in_=bias_ps[i][:])

        def add_bias(eng, j, i, a0, na, pool=False):
            r3 = r_t[j][:].rearrange("p (a n) -> p a n", a=2)
            s = slice(HALF * i, HALF * (i + 1))
            row = (bias_sb[:, s] if pool else bias_ps[i][:]).rearrange("p (b n) -> p b n", b=2).unsqueeze(1).to_broadcast([P, na, 2, 256])
            rec = r3[:, a0:a0 + na, s].rearrange("p a (b n) -> p a b n", b=2)
            eng.tensor_tensor(
                out=half(2 * j + a0, na, i),
                in0=rec if pool else row,
                in1=row if pool else rec,
                op=ALU.add,
            )

        def bias_matmul(j, a, i=1):
            s = slice(HALF * i, HALF * (i + 1))
            pre = psum.tile([P, HALF], F32, tag="tp", bufs=2, name="pre")
            pre_t[(j, a, i)] = pre
            nc.tensor.matmul(pre[:], lhsT=identb[:], rhs=r_t[j][:, a * N + HALF * i:a * N + HALF * (i + 1)], start=True, stop=False)
            nc.tensor.matmul(pre[:], lhsT=ones[:], rhs=brow[:, s], start=False, stop=True)

        def bias_copy(j, a, i=1):
            nc.scalar.copy(out=half(2 * j + a, 1, i)[:, 0], in_=pre_t[(j, a, i)][:].rearrange("p (b n) -> p b n", b=2))

        def four_transposes(out, words):
            for jj in range(4):
                lo = 256 * (jj // 2) + jj % 2
                nc.tensor.transpose(out[:, P * jj:P * (jj + 1)], words[:, lo:256 * (jj // 2 + 1):2], ident[:])

        def transposes(j, a):
            tp_t[(j, a)] = psum.tile([P, HALF], F32, tag="tp", bufs=2, name="tp")
            four_transposes(tp_t[(j, a)], h_t[j][:].bitcast(F32)[:, 512 * a:512 * (a + 1)])

        def regroup(j, a, eng="S"):
            q = j // 2
            if q not in gq_t:
                gq_t[q] = work.tile([P, 4 * K], BF16, tag="gq", bufs=3, name="gq", align_bytes=64)
            gq_w = gq_t[q][:].bitcast(F32).rearrange("p (t g r u) -> p t g r u", t=4, g=2, u=2)
            src = tp_t[(j, a)][:].rearrange("p (g u r) -> p g r u", g=2, u=2)
            if eng == "V":
                nc.vector.tensor_copy(out=gq_w[:, (2 * j) % 4 + a], in_=src)
            else:
                nc.scalar.copy(out=gq_w[:, (2 * j) % 4 + a], in_=src)

        def quantise(t0, nt):
            q = t0 // 4
            if q not in hc_t:
                hc_t[q] = work.tile([P, 1024], U32, tag="hc", name="hc", align_bytes=64)
                hs_t[q] = work.tile([P, 1024], U8, tag="hs", name="hs", align_bytes=64)
            s = slice(t0 % 4 * 256, (t0 % 4 + nt) * 256)
            nc.vector.quantize_mx(out=hc_t[q][:, s].bitcast(FP8X4), scales=hs_t[q][:, s], in_=gq_t[q][:, t0 % 4 * K:(t0 % 4 + nt) * K])

        wtp_t = {}

        def w_transposes(a):
            wtp_t[a] = psum.tile([P, HALF], F32, tag="acc", bufs=4, name="wtp")
            four_transposes(wtp_t[a], w_t[0][:].bitcast(F32)[:, 512 * a:512 * (a + 1)])

        def w_regroup(a, eng):
            half = a // 4
            if 0 not in wq_t:
                wq_t[0] = work.tile([P, 8 * K], BF16, tag="x", bufs=XB, name="wq", align_bytes=64)
            dst = wq_t[0][:, half * 4 * K:(half + 1) * 4 * K].bitcast(F32).rearrange("p (g n u) -> p g n u", g=2, u=2)[:, :, P * (a % 4):P * (a % 4 + 1), :]
            src = wtp_t[a][:].rearrange("p (g u r) -> p g r u", g=2, u=2)
            if eng == "V":
                nc.vector.tensor_copy(out=dst, in_=src)
            else:
                nc.scalar.copy(out=dst, in_=src)

        def w_quantise(half):
            s = slice(half * N, (half + 1) * N)
            nc.vector.quantize_mx(out=wc[:, s].bitcast(FP8X4), scales=ws[:, s], in_=wq_t[0][:, half * 4 * K:(half + 1) * 4 * K])

        def project(j, a, nh):
            acc = psum.tile([P, HALF], F32, tag="acc", bufs=4, name="acc")
            acc_t[(j, a, nh)] = acc
            for g in range(2):
                lo = (((2 * j) % 4 + a) * 2 + g) * P
                wlo = nh * N + g * HALF
                nc.tensor.matmul_mx(
                    out=acc[:],
                    lhsT=hc_t[j // 2][:, lo:lo + P].bitcast(FP8X4),
                    lhsT_scale=hs_t[j // 2][:, lo:lo + P],
                    rhs=wc[:, wlo:wlo + HALF].bitcast(FP8X4),
                    rhs_scale=ws[:, wlo:wlo + HALF],
                    start=(g == 0),
                    stop=(g == 1),
                )

        def add_proj(j, a, nh):
            dst = half(2 * j + a, 1, nh)[:, 0]
            nc.vector.tensor_tensor(out=dst, in0=acc_t[(j, a, nh)][:].rearrange("p (b n) -> p b n", b=2), in1=dst, op=ALU.add)

        def sl(t0, nt):
            return slice(t0 % 4, t0 % 4 + nt)

        def act(t0, nt, lo, hi, func):
            x = x3(t0)[:, sl(t0, nt), lo:hi]
            nc.scalar.activation(out=x, in_=x, func=func)

        def out3(tiles, t0, tag):
            q = t0 // 4
            if q not in tiles:
                tiles[q] = work.tile([P, 4 * H], F32, tag=tag, bufs=3, name=tag + "_sb")
            return tiles[q][:].rearrange("p (a n) -> p a n", a=4)

        def cell_f(eng, t0, nt):
            x = x3(t0)[:, sl(t0, nt), 512:768]
            c3 = c_t[t0 // 4][:].rearrange("p (a n) -> p a n", a=4)
            eng.tensor_tensor(out=x, in0=x, in1=c3[:, sl(t0, nt), :], op=ALU.mult)

        def cell_i(eng, t0, nt):
            x = x3(t0)[:, sl(t0, nt), :]
            eng.tensor_tensor(out=x[:, :, 256:512], in0=x[:, :, 256:512], in1=x[:, :, 0:256], op=ALU.mult)

        def cell_add(eng, t0, nt):
            x = x3(t0)[:, sl(t0, nt), :]
            eng.tensor_tensor(out=out3(cn_t, t0, "cn")[:, sl(t0, nt), :], in0=x[:, :, 256:512], in1=x[:, :, 512:768], op=ALU.add)

        def cell_tanh(t0, nt):
            x = x3(t0)[:, sl(t0, nt), 0:256]
            nc.scalar.activation(out=x, in_=out3(cn_t, t0, "cn")[:, sl(t0, nt), :], func=ACT.Tanh)

        def hidden(eng, t0, nt):
            x = x3(t0)[:, sl(t0, nt), :]
            eng.tensor_tensor(out=out3(hn_t, t0, "hn")[:, sl(t0, nt), :], in0=x[:, :, 768:1024], in1=x[:, :, 0:256], op=ALU.mult)

        def store(dram, tiles, t0, nt):
            lo = (t0 % 4) * H
            nc.sync.dma_start(out=dram[:, t0 * H:(t0 + nt) * H], in_=tiles[t0 // 4][:, lo:lo + nt * H])

        V, G = nc.vector, nc.gpsimd

        def cells(eng, t0, nt):
            cell_f(eng, t0, nt)
            cell_i(eng, t0, nt)
            cell_add(eng, t0, nt)

        def tanh_c(t0, nt):
            cell_tanh(t0, nt)
            store(oc_v, cn_t, t0, nt)

        def out_h(t0, nt):
            hidden(V, t0, nt)
            store(oh_v, hn_t, t0, nt)

        def load(what):
            {"h": load_h, "r": load_rec, "w": load_w, "c": load_c}[what[0]](int(what[1:]))

        def two(fn, j):
            for a in range(2):
                fn(j, a)

        for what in ORDER.split():
            load(what)

        def bias_all(j):
            if j in GP:
                for i in range(2):
                    for a in range(2):
                        add_bias(G, j, i, a, 1, True)
            else:
                for i in range(2):
                    add_bias(V, j, i, 0, 2)

        def w_block(a):
            w_transposes(a)
            w_regroup(a, "V" if a in WV else "S")

        for what in HEAD.split():
            kind, n = what[0], int(what[1:] or 0)
            if kind == "R":
                bias_rows(n)
            if kind == "O":
                bias_out(n)
            if kind == "T":
                two(transposes, n)
            if kind == "g":
                for a in range(2):
                    regroup(n, a, V_G if n == 0 else "S")
            if kind == "B":
                bias_all(n)
            if kind == "Q":
                quantise(n // 10, n % 10)
            if kind == "w":
                w_transposes(n)
            if kind == "k":
                w_regroup(n, "V" if n in WV else "S")
            if kind == "W":
                w_quantise(n)
            if kind == "M":
                project(0, n // 10, n % 10)
            if kind == "A":
                add_proj(0, n // 10, n % 10)

        for j in range(NPAIR):
            q = j // 2
            even = j % 2 == 0
            more = j + 1 < NPAIR
            jb = j + 2
            bias = jb < NPAIR and jb not in GP
            pe = [[], [1], [0, 1]][PN[jb]] if bias else []
            if j + 4 < NPAIR:
                load_rec(j + 4)
            if j + R + 2 < NPAIR:
                load_h(j + R + 2)
            if even and q + 2 < NPAIR // 2:
                load_c(q + 2)

            if j + R < NPAIR:
                two(regroup, j + R)
            if j > 0:
                add_proj(j, 0, 0)
            if more:
                project(j + 1, 0, 0)
            for a in pe:
                bias_matmul(jb, a)
            for what in SO:
                if what == "T" and j > 0 and not TQ:
                    act(2 * j - 2, 2, 0, 256, ACT.Tanh)
                if what == "T" and even and j > 0 and TQ:
                    act(2 * j - 4, 4, 0, 256, ACT.Tanh)
                if what == "T" and j == 15 and TQ:
                    act(28, 2, 0, 256, ACT.Tanh)
                if what == "S" and j > 0:
                    act(2 * j - 2, 2, 256, 1024, ACT.Sigmoid)
                if what == "0" and pe:
                    bias_copy(jb, pe[0])
                if what == "1" and len(pe) > 1:
                    bias_copy(jb, pe[1])
            if even and 1 <= q <= CG:
                fv = F6 if q == 7 else F5 if q == 6 else FV
                if fv < 4:
                    cell_f(G, 4 * q - 4 + fv, 4 - fv)
                cell_i(G, 4 * q - 4, 4)
            def run():
                for what in RO:
                    if what == "h" and even and q >= 3:
                        out_h(4 * (q - 3), 4)
                    if what == "f" and even and 1 <= q <= CG and fv:
                        cell_f(V, 4 * q - 4, fv)
                    if what == "q" and j < 2:
                        quantise(4 + 2 * j, 2)
                    elif what == "q" and even and q + 1 < NPAIR // 2:
                        quantise(4 * q + 4, 4)
            rn = (R0, R1)[j] if j < 2 else R14 if j == 14 else RUN
            if rn == 0:
                run()
            if bias:
                add_bias(V, jb, 0, 0, 2)
            if rn == 1:
                run()
            add_proj(j, 0, 1)
            if more:
                project(j + 1, 0, 1)
            if rn == 2:
                run()
            if j > 0:
                add_proj(j, 1, 0)
            if more:
                project(j + 1, 1, 0)
            if bias and len(pe) < 2:
                add_bias(V, jb, 1, 0, 1 if pe else 2)
            if rn == 3:
                run()
            add_proj(j, 1, 1)
            if rn == 4:
                run()
            if TPOS == 3 and j + R + 1 < NPAIR:
                two(transposes, j + R + 1)
            if more:
                project(j + 1, 1, 1)
            if TPOS == 4 and j + R + 1 < NPAIR:
                two(transposes, j + R + 1)
            if even and 1 <= q <= CG and not (q == 7 and A6 == "V"):
                cell_add(G, 4 * q - 4, 4)
            if even and q >= 2:
                tanh_c(4 * (q - 2), 4)

        for t in (30, 31):
            act(t, 1, 0, 256, ACT.Tanh)
            act(t, 1, 256, 1024, ACT.Sigmoid)
        for what in TAIL.split():
            kind, t0, nt = what[0], int(what[1:3]), int(what[3:])
            if kind == "a":
                cell_add(V, t0, nt)
            if kind == "c":
                cells(V, t0, nt)
            if kind == "f":
                cell_f(V, t0, nt)
            if kind == "i":
                cell_i(V, t0, nt)
            if kind == "t":
                tanh_c(t0, nt)
            if kind == "h":
                out_h(t0, nt)
